import numpy as np
import ml_dtypes


def mxq(x, axis, fmt="e4m3"):
    dtype, down = {"e4m3": (ml_dtypes.float8_e4m3fn, 7), "e5m2": (ml_dtypes.float8_e5m2, 14)}[fmt]
    v = np.moveaxis(np.asarray(x, np.float32).astype(ml_dtypes.bfloat16).astype(np.float64), axis, -1)
    blocks = v.reshape(v.shape[:-1] + (-1, 32))
    amax = np.abs(blocks).max(-1, keepdims=True)
    byte = np.maximum(np.where(amax > 0, np.frexp(amax)[1] - 1 + 127, 0) - down, 1)
    scale = np.exp2(byte - 127.0)
    codes = (blocks / scale).astype(np.float32).astype(dtype).astype(np.float64)
    return np.moveaxis((codes * scale).reshape(v.shape), -1, axis)


WIDE = False


def mx_kscale(k):
    if not WIDE:
        return np.ones(k)
    levels = np.array([10, -10, 5, -5, 0])
    if k % 512:
        return np.exp2(np.random.permutation(np.resize(levels, k // 32))).repeat(32)
    a = np.empty((k // 512, 16))
    for p in range(k // 512):
        a[p, :8] = np.random.permutation(np.resize(levels, 8))
        for g in range(8):
            far = levels[np.abs(levels - a[p, g]) >= 10]
            a[p, g + 8] = far[np.random.randint(len(far))]
    return np.exp2(a.ravel()).repeat(32)


BF16 = ml_dtypes.bfloat16


def bf(x):
    return np.asarray(x, np.float32).astype(BF16)


def f64(x):
    return np.asarray(x).astype(np.float64)


B, D, A = 6144, 512, 128


def setup_inputs():
    s = mx_kscale(D)
    return {
        "x": bf(np.random.standard_normal((B, D)) * s),
        "saved_x": bf(np.random.standard_normal((B, D)) * s),
        "saved_a": bf(np.random.standard_normal((B, A))),
        "saved_b": bf(0.5 + np.random.random((B, A))),
        "saved_p": bf(np.random.standard_normal((B, A))),
        "time_decay": bf(np.random.standard_normal(A)),
        "time_first": bf(np.random.standard_normal(A)),
        "k_mixed": bf(np.random.random(D)),
        "v_mixed": bf(np.random.random(D)),
        "key_weight": bf(np.random.standard_normal((D, A)) / np.sqrt(D) / s[:, None]),
        "value_weight": bf(np.random.standard_normal((D, A)) / np.sqrt(D) / s[:, None]),
    }


def reference(x, saved_x, saved_a, saved_b, saved_p, time_decay, time_first, k_mixed, v_mixed, key_weight, value_weight):
    x, saved_x = f64(x), f64(saved_x)
    saved_a, saved_b, saved_p = f64(saved_a), f64(saved_b), f64(saved_p)
    time_decay, time_first = f64(time_decay), f64(time_first)
    k_mixed, v_mixed = f64(k_mixed), f64(v_mixed)
    xk = x * k_mixed + saved_x * (1.0 - k_mixed)
    xv = x * v_mixed + saved_x * (1.0 - v_mixed)
    k = mxq(xk, 1, "e4m3") @ mxq(f64(key_weight), 0, "e4m3")
    v = mxq(xv, 1, "e4m3") @ mxq(f64(value_weight), 0, "e4m3")
    w = k + time_first
    p = np.maximum(saved_p, w)
    e1 = np.exp(saved_p - p)
    e2 = np.exp(w - p)
    wkv = (e1 * saved_a + e2 * v) / (e1 * saved_b + e2)
    w2 = saved_p + time_decay
    p2 = np.maximum(w2, k)
    f1 = np.exp(w2 - p2)
    f2 = np.exp(k - p2)
    aa = f1 * saved_a + f2 * v
    bb = f1 * saved_b + f2
    return wkv, aa, bb, p2

@@ -1,0 +1,341 @@
+from contextlib import ExitStack
+
+import concourse.mybir as mybir
+from concourse.masks import make_identity
+
+F32 = mybir.dt.float32
+BF16 = mybir.dt.bfloat16
+U32 = mybir.dt.uint32
+U8 = mybir.dt.uint8
+FP8X4 = mybir.dt.float8_e4m3fn_x4
+ALU = mybir.AluOpType
+ACT = mybir.ActivationFunctionType
+
+P = 128
+B, D, A = 6144, 512, 128
+PACK = 4
+HALVES = 2
+PAIR = 2
+ROWS_PER_PARTITION = B // P
+TILES = 4
+GROUP = TILES * P
+GROUPS = B // GROUP
+VECTOR_TILES = 1
+LN_BATCH = 5
+
+FLOPS = 2 * 2 * B * D * A
+
+
+def tile_rwkv_attention_pa_t_kernel(
+    tc,
+    x,
+    saved_x,
+    saved_a,
+    saved_b,
+    saved_p,
+    time_decay,
+    time_first,
+    k_mixed,
+    v_mixed,
+    key_weight,
+    value_weight,
+    wkv_out,
+    aa_out,
+    bb_out,
+    p2_out,
+):
+    nc = tc.nc
+
+    def by_partition(dram):
+        return dram.rearrange("(p n) c -> p n c", n=ROWS_PER_PARTITION)
+
+    x_rows, sx_rows = by_partition(x), by_partition(saved_x)
+    sa_rows, sb_rows, sp_rows = by_partition(saved_a), by_partition(saved_b), by_partition(saved_p)
+    wkv_rows, aa_rows = by_partition(wkv_out), by_partition(aa_out)
+    bb_rows, p2_rows = by_partition(bb_out), by_partition(p2_out)
+
+    def rows_of(g):
+        return slice(g * TILES, (g + 1) * TILES)
+
+    def in_range(g):
+        return 0 <= g < GROUPS
+
+    with ExitStack() as stack:
+        const = stack.enter_context(tc.tile_pool(name="const", bufs=1))
+        sbuf = stack.enter_context(tc.tile_pool(name="sbuf", bufs=2))
+        psum = stack.enter_context(tc.psum_pool(name="psum", bufs=1))
+        stack.enter_context(tc.manual_schedule())
+
+        identity = const.tile([P, P], F32, name="identity")
+        make_identity(nc, identity[:])
+
+        mix_rows = const.tile([P, D], BF16, name="mix_rows")
+        nc.vector.memset(mix_rows[:], 0.0)
+        nc.scalar.dma_start(out=mix_rows[0:1, :], in_=k_mixed.unsqueeze(0))
+        nc.scalar.dma_start(out=mix_rows[1:2, :], in_=v_mixed.unsqueeze(0))
+
+        w_raw = const.tile([P, 2, PACK, A], BF16, name="w_raw")
+        for c, weight in enumerate((key_weight, value_weight)):
+            nc.scalar.dma_start(
+                out=w_raw[:, c], in_=weight.rearrange("(q t) a -> q t a", t=PACK)
+            )
+        decay_bc = const.tile([P, A], BF16, name="decay_bc")
+        first_bc = const.tile([P, A], BF16, name="first_bc")
+        nc.scalar.dma_start(out=decay_bc[:], in_=time_decay.partition_broadcast(P))
+        nc.scalar.dma_start(out=first_bc[:], in_=time_first.partition_broadcast(P))
+
+        mix_t = psum.tile([P, GROUP], F32, name="mix_t", tag="x_t0")
+        for u in range(HALVES):
+            nc.tensor.transpose(
+                out=mix_t[:, u * P : (u + 1) * P],
+                in_=mix_rows[:].bitcast(F32)[:, u::HALVES],
+                identity=identity[:],
+            )
+        mix = const.tile([P, 2, PACK], F32, name="mix")
+        for u in range(HALVES):
+            first_column = u * P * PAIR
+            nc.vector.tensor_copy(
+                out=mix[:, :, PAIR * u : PAIR * (u + 1)],
+                in_=mix_t[:]
+                .bitcast(BF16)[:, first_column : first_column + 2 * PAIR]
+                .rearrange("q (c e) -> q c e", e=PAIR),
+            )
+        one_minus_mix = const.tile([P, 2, PACK], F32, name="one_minus_mix")
+        nc.vector.tensor_scalar(
+            out=one_minus_mix[:], in0=mix[:], scalar1=-1.0, scalar2=1.0, op0=ALU.mult, op1=ALU.add
+        )
+
+        w_grouped = const.tile([P, 2, A, PACK], BF16, name="w_grouped", align_bytes=64)
+        for c in range(2):
+            nc.vector.tensor_copy(out=w_grouped[:, c], in_=w_raw[:, c].rearrange("q t a -> q a t"))
+        w_codes = const.tile([P, 2 * A], U32, name="w_codes", align_bytes=64)
+        w_scales = const.tile([P, 2 * A], U8, name="w_scales", align_bytes=64)
+        nc.vector.quantize_mx(
+            out=w_codes[:].bitcast(FP8X4),
+            scales=w_scales[:],
+            in_=w_grouped[:].rearrange("q c a t -> q (c a t)"),
+        )
+
+        first_plus_decay = const.tile([P, A], F32, name="first_plus_decay")
+        nc.vector.tensor_tensor(
+            out=first_plus_decay[:], in0=first_bc[:], in1=decay_bc[:], op=ALU.add
+        )
+        two = const.tile([P, 1], F32, name="two")
+        nc.vector.memset(two[:], 2.0)
+
+        def over_tiles(row):
+            return row[:].unsqueeze(1).to_broadcast([P, TILES, A])
+
+        sa_all = const.tile([P, ROWS_PER_PARTITION, A], BF16, name="sa_all")
+        sb_all = const.tile([P, ROWS_PER_PARTITION, A], BF16, name="sb_all")
+        sp_all = const.tile([P, ROWS_PER_PARTITION, A], BF16, name="sp_all")
+
+        live = {}
+
+        def new(name, g, shape, dtype, bufs, pool=sbuf, align_bytes=None):
+            live[name, g] = pool.tile(
+                shape, dtype, name="%s_%d" % (name, g), tag=name, bufs=bufs, align_bytes=align_bytes
+            )
+            return live[name, g]
+
+        def new_f32(name, g, bufs):
+            return new(name, g, [P, TILES, A], F32, bufs)
+
+        def load(g):
+            if not in_range(g):
+                return
+            nc.sync.dma_start(out=new("sx", g, [P, TILES, D], BF16, 3)[:], in_=sx_rows[:, rows_of(g), :])
+            nc.sync.dma_start(out=new("x", g, [P, TILES, D], BF16, 3)[:], in_=x_rows[:, rows_of(g), :])
+            nc.sync.dma_start(out=sp_all[:, rows_of(g), :], in_=sp_rows[:, rows_of(g), :])
+            nc.sync.dma_start(out=sb_all[:, rows_of(g), :], in_=sb_rows[:, rows_of(g), :])
+            nc.sync.dma_start(out=sa_all[:, rows_of(g), :], in_=sa_rows[:, rows_of(g), :])
+
+        def transpose(name, g):
+            if not in_range(g):
+                return
+            words = live[name, g][:].bitcast(F32)
+            for u in range(HALVES):
+                bank = new("%s_t%d" % (name, u), g, [P, GROUP], F32, 1, pool=psum)
+                for j in range(TILES):
+                    nc.tensor.transpose(
+                        out=bank[:, j * P : (j + 1) * P],
+                        in_=words[:, j, u::HALVES],
+                        identity=identity[:],
+                    )
+
+        def value_of_word(name, g, t):
+            u, e = divmod(t, PAIR)
+            bank = live["%s_t%d" % (name, u), g]
+            return bank[:].bitcast(BF16).rearrange("q (r e) -> q e r", e=PAIR)[:, e, :]
+
+        def scale_saved_x(g):
+            if not in_range(g):
+                return
+            for c in range(2):
+                new("scaled%d" % c, g, [P, PACK, GROUP], F32, 2)
+            for t in range(PACK):
+                for c in range(2):
+                    nc.scalar.activation(
+                        out=live["scaled%d" % c, g][:, t, :],
+                        in_=value_of_word("sx", g, t),
+                        func=ACT.Copy,
+                        scale=one_minus_mix[:, c, t : t + 1],
+                    )
+
+        def mix_x(g):
+            if not in_range(g):
+                return
+            for c in range(2):
+                new("mixed%d" % c, g, [P, PACK, GROUP], BF16, 2)
+            for t in range(PACK):
+                for c in range(2):
+                    nc.vector.scalar_tensor_tensor(
+                        out=live["mixed%d" % c, g][:, t, :],
+                        in0=value_of_word("x", g, t),
+                        scalar=mix[:, c, t : t + 1],
+                        in1=live["scaled%d" % c, g][:, t, :],
+                        op0=ALU.mult,
+                        op1=ALU.add,
+                    )
+
+        def group_words(g, engine_copy, first_tile, last_tile):
+            if not in_range(g):
+                return
+            rows = slice(first_tile * P, last_tile * P)
+            for c in range(2):
+                if ("grouped%d" % c, g) not in live:
+                    new("grouped%d" % c, g, [P, GROUP, PACK], BF16, 1, align_bytes=64)
+                engine_copy(
+                    out=live["grouped%d" % c, g][:, rows, :].rearrange("q (n i) t -> q n t i", i=4),
+                    in_=live["mixed%d" % c, g][:, :, rows].rearrange("q t (n i) -> q n t i", i=4),
+                )
+
+        def quantise(g):
+            if not in_range(g):
+                return
+            for c in range(2):
+                codes = new("codes%d" % c, g, [P, GROUP], U32, 2, align_bytes=64)
+                scales = new("scales%d" % c, g, [P, GROUP], U8, 2, align_bytes=64)
+                nc.vector.quantize_mx(
+                    out=codes[:].bitcast(FP8X4),
+                    scales=scales[:],
+                    in_=live["grouped%d" % c, g][:].rearrange("q r t -> q (r t)"),
+                )
+
+        def project(g):
+            if not in_range(g):
+                return
+            for c, (name, bufs) in enumerate((("k", 1), ("v", 2))):
+                bank = new(name, g, [P, TILES, A], F32, bufs, pool=psum)
+                for j in range(TILES):
+                    tile_rows = slice(j * P, (j + 1) * P)
+                    nc.tensor.matmul_mx(
+                        out=bank[:, j, :],
+                        lhsT=live["codes%d" % c, g][:, tile_rows].bitcast(FP8X4),
+                        lhsT_scale=live["scales%d" % c, g][:, tile_rows],
+                        rhs=w_codes[:, c * A : (c + 1) * A].bitcast(FP8X4),
+                        rhs_scale=w_scales[:, c * A : (c + 1) * A],
+                        start=True,
+                        stop=True,
+                    )
+
+        def prepare_state(g):
+            if not in_range(g):
+                return
+            nc.gpsimd.tensor_tensor(
+                out=new_f32("w2", g, 2)[:], in0=sp_all[:, rows_of(g), :], in1=over_tiles(decay_bc), op=ALU.add
+            )
+            nc.gpsimd.tensor_scalar(
+                out=new_f32("one_minus_sb", g, 3)[:],
+                in0=sb_all[:, rows_of(g), :],
+                scalar1=-1.0,
+                scalar2=1.0,
+                op0=ALU.mult,
+                op1=ALU.add,
+            )
+
+        def compare(g):
+            if not in_range(g):
+                return
+            k, v, w2 = live["k", g], live["v", g], live["w2", g]
+            nc.vector.tensor_tensor(out=new_f32("d2", g, 2)[:], in0=k[:], in1=w2[:], op=ALU.subtract)
+            nc.vector.tensor_tensor(out=new_f32("p2", g, 2)[:], in0=k[:], in1=w2[:], op=ALU.max)
+            nc.vector.tensor_tensor(
+                out=new_f32("v_minus_sa", g, 2)[:], in0=v[:], in1=sa_all[:, rows_of(g), :], op=ALU.subtract
+            )
+            nc.sync.dma_start(out=p2_rows[:, rows_of(g), :], in_=live["p2", g][:])
+            nc.gpsimd.tensor_tensor(
+                out=new_f32("d", g, 2)[:], in0=live["d2", g][:], in1=over_tiles(first_plus_decay), op=ALU.add
+            )
+
+        def exponentials(g):
+            if not in_range(g):
+                return
+            d2, d = live["d2", g], live["d", g]
+            nc.scalar.activation(out=new_f32("exp_up", g, 2)[:], in_=d2[:], func=ACT.Exp)
+            nc.scalar.activation(out=new_f32("exp_down", g, 2)[:], in_=d2[:], func=ACT.Exp, scale=-1.0)
+            nc.scalar.activation(out=new_f32("th", g, 2)[:], in_=d[:], func=ACT.Tanh, scale=0.5)
+
+        def blend(g):
+            if not in_range(g):
+                return
+            sa, sb = sa_all[:, rows_of(g), :], sb_all[:, rows_of(g), :]
+            v, th, up, down = live["v", g], live["th", g], live["exp_up", g], live["exp_down", g]
+            stt = nc.vector.scalar_tensor_tensor
+            pull, num, f1_sb = new_f32("pull", g, 1), new_f32("num", g, 1), new_f32("f1_sb", g, 1)
+            f1_sa, f2_v = new_f32("f1_sa", g, 2), new_f32("f2_v", g, 2)
+            den_minus_2, num_den = new_f32("den_minus_2", g, 2), new_f32("num_den", g, LN_BATCH + 1)
+            aa, bb = new_f32("aa", g, 2), new_f32("bb", g, 2)
+            stt(out=den_minus_2[:], in0=th[:], scalar=1.0, in1=live["one_minus_sb", g][:], op0=ALU.subtract, op1=ALU.mult)
+            stt(out=pull[:], in0=th[:], scalar=1.0, in1=live["v_minus_sa", g][:], op0=ALU.subtract, op1=ALU.mult)
+            stt(out=f2_v[:], in0=up[:], scalar=1.0, in1=v[:], op0=ALU.min, op1=ALU.mult)
+            stt(out=num[:], in0=v[:], scalar=2.0, in1=pull[:], op0=ALU.mult, op1=ALU.add)
+            stt(out=f1_sa[:], in0=down[:], scalar=1.0, in1=sa, op0=ALU.min, op1=ALU.mult)
+            stt(out=f1_sb[:], in0=down[:], scalar=1.0, in1=sb, op0=ALU.min, op1=ALU.mult)
+            stt(out=num_den[:], in0=den_minus_2[:], scalar=2.0, in1=num[:], op0=ALU.add, op1=ALU.mult)
+            stt(out=bb[:], in0=up[:], scalar=1.0, in1=f1_sb[:], op0=ALU.min, op1=ALU.add)
+            nc.gpsimd.tensor_tensor(out=aa[:], in0=f1_sa[:], in1=f2_v[:], op=ALU.add)
+            nc.sync.dma_start(out=aa_rows[:, rows_of(g), :], in_=aa[:])
+            nc.sync.dma_start(out=bb_rows[:, rows_of(g), :], in_=bb[:])
+
+        def square_den(g):
+            if not in_range(g):
+                return
+            nc.scalar.activation(
+                out=new_f32("inv_den2", g, LN_BATCH)[:], in_=live["den_minus_2", g][:], func=ACT.Square, bias=two[:, 0:1]
+            )
+
+        def batch_ending_at(g):
+            if in_range(g) and ((g + 1) % LN_BATCH == 0 or g == GROUPS - 1):
+                return range(g // LN_BATCH * LN_BATCH, g + 1)
+            return range(0)
+
+        def invert_den2(last):
+            for g in batch_ending_at(last):
+                nc.scalar.activation(out=live["inv_den2", g][:], in_=live["inv_den2", g][:], func=ACT.Ln)
+            for g in batch_ending_at(last):
+                nc.scalar.activation(out=live["inv_den2", g][:], in_=live["inv_den2", g][:], func=ACT.Exp, scale=-1.0)
+
+        def divide(last):
+            for g in batch_ending_at(last):
+                wkv = new_f32("wkv", g, 3)
+                nc.gpsimd.tensor_tensor(out=wkv[:], in0=live["num_den", g][:], in1=live["inv_den2", g][:], op=ALU.mult)
+                nc.sync.dma_start(out=wkv_rows[:, rows_of(g), :], in_=wkv[:])
+
+        for i in range(-2, GROUPS + 4):
+            load(i + 2)
+            scale_saved_x(i)
+            transpose("sx", i + 1)
+            group_words(i - 1, nc.vector.tensor_copy, 0, VECTOR_TILES)
+            blend(i - 3)
+            compare(i - 2)
+            divide(i - 4)
+            prepare_state(i - 1)
+            mix_x(i)
+            transpose("x", i + 1)
+            group_words(i - 1, nc.scalar.copy, VECTOR_TILES, TILES)
+            quantise(i - 1)
+            project(i - 1)
+            square_den(i - 3)
+            exponentials(i - 2)
+            invert_den2(i - 3)

@@ -20,7 +20,7 @@ ROWS_PER_PARTITION = B // P
 TILES = 4
 GROUP = TILES * P
 GROUPS = B // GROUP
-VECTOR_TILES = 1
+RATIO_MAX = 2.0**32
 LN_BATCH = 5
 
 FLOPS = 2 * 2 * B * D * A
@@ -120,14 +120,13 @@ def tile_rwkv_attention_pa_t_kernel(
         nc.vector.tensor_tensor(
             out=first_plus_decay[:], in0=first_bc[:], in1=decay_bc[:], op=ALU.add
         )
-        two = const.tile([P, 1], F32, name="two")
-        nc.vector.memset(two[:], 2.0)
+        one = const.tile([P, 1], F32, name="one")
+        nc.vector.memset(one[:], 1.0)
 
         def over_tiles(row):
             return row[:].unsqueeze(1).to_broadcast([P, TILES, A])
 
-        sa_all = const.tile([P, ROWS_PER_PARTITION, A], BF16, name="sa_all")
-        sb_all = const.tile([P, ROWS_PER_PARTITION, A], BF16, name="sb_all")
+        sab_all = const.tile([P, GROUPS, 2, TILES * A], BF16, name="sab_all")
         sp_all = const.tile([P, ROWS_PER_PARTITION, A], BF16, name="sp_all")
 
         live = {}
@@ -147,39 +146,60 @@ def tile_rwkv_attention_pa_t_kernel(
             nc.sync.dma_start(out=new("sx", g, [P, TILES, D], BF16, 3)[:], in_=sx_rows[:, rows_of(g), :])
             nc.sync.dma_start(out=new("x", g, [P, TILES, D], BF16, 3)[:], in_=x_rows[:, rows_of(g), :])
             nc.sync.dma_start(out=sp_all[:, rows_of(g), :], in_=sp_rows[:, rows_of(g), :])
-            nc.sync.dma_start(out=sb_all[:, rows_of(g), :], in_=sb_rows[:, rows_of(g), :])
-            nc.sync.dma_start(out=sa_all[:, rows_of(g), :], in_=sa_rows[:, rows_of(g), :])
+            for which, rows in enumerate((sa_rows, sb_rows)):
+                nc.sync.dma_start(
+                    out=sab_all[:, g, which].rearrange("p (j a) -> p j a", a=A), in_=rows[:, rows_of(g), :]
+                )
 
-        def transpose(name, g):
+        def transpose(name, g, u):
             if not in_range(g):
                 return
             words = live[name, g][:].bitcast(F32)
-            for u in range(HALVES):
-                bank = new("%s_t%d" % (name, u), g, [P, GROUP], F32, 1, pool=psum)
-                for j in range(TILES):
-                    nc.tensor.transpose(
-                        out=bank[:, j * P : (j + 1) * P],
-                        in_=words[:, j, u::HALVES],
-                        identity=identity[:],
-                    )
+            bank = new("%s_t%d" % (name, u), g, [P, GROUP], F32, 1, pool=psum)
+            for j in range(TILES):
+                nc.tensor.transpose(
+                    out=bank[:, j * P : (j + 1) * P],
+                    in_=words[:, j, u::HALVES],
+                    identity=identity[:],
+                )
 
-        def value_of_word(name, g, t):
-            u, e = divmod(t, PAIR)
-            bank = live["%s_t%d" % (name, u), g]
+        def value_of_word(bank, e):
             return bank[:].bitcast(BF16).rearrange("q (r e) -> q e r", e=PAIR)[:, e, :]
 
-        def scale_saved_x(g):
+        def scale_on_scalar(g):
             if not in_range(g):
                 return
             for c in range(2):
-                new("scaled%d" % c, g, [P, PACK, GROUP], F32, 2)
-            for t in range(PACK):
+                new("scaled%d0" % c, g, [P, PAIR, GROUP], F32, 2)
+            for e in range(PAIR):
                 for c in range(2):
                     nc.scalar.activation(
-                        out=live["scaled%d" % c, g][:, t, :],
-                        in_=value_of_word("sx", g, t),
+                        out=live["scaled%d0" % c, g][:, e, :],
+                        in_=value_of_word(live["sx_t0", g], e),
                         func=ACT.Copy,
-                        scale=one_minus_mix[:, c, t : t + 1],
+                        scale=one_minus_mix[:, c, e : e + 1],
+                    )
+
+        def fetch_words(g):
+            if not in_range(g):
+                return
+            nc.scalar.copy(out=new("sx_words", g, [P, GROUP], F32, 2)[:], in_=live["sx_t1", g][:])
+
+        def scale_on_gpsimd(g):
+            if not in_range(g):
+                return
+            for c in range(2):
+                new("scaled%d1" % c, g, [P, PAIR, GROUP], F32, 2)
+            for e in range(PAIR):
+                for c in range(2):
+                    t = PAIR + e
+                    nc.gpsimd.tensor_scalar(
+                        out=live["scaled%d1" % c, g][:, e, :],
+                        in0=value_of_word(live["sx_words", g], e),
+                        scalar1=one_minus_mix[:, c, t : t + 1],
+                        scalar2=0.0,
+                        op0=ALU.mult,
+                        op1=ALU.add,
                     )
 
         def mix_x(g):
@@ -188,26 +208,26 @@ def tile_rwkv_attention_pa_t_kernel(
             for c in range(2):
                 new("mixed%d" % c, g, [P, PACK, GROUP], BF16, 2)
             for t in range(PACK):
+                u, e = divmod(t, PAIR)
                 for c in range(2):
                     nc.vector.scalar_tensor_tensor(
                         out=live["mixed%d" % c, g][:, t, :],
-                        in0=value_of_word("x", g, t),
+                        in0=value_of_word(live["x_t%d" % u, g], e),
                         scalar=mix[:, c, t : t + 1],
-                        in1=live["scaled%d" % c, g][:, t, :],
+                        in1=live["scaled%d%d" % (c, u), g][:, e, :],
                         op0=ALU.mult,
                         op1=ALU.add,
                     )
 
-        def group_words(g, engine_copy, first_tile, last_tile):
+        def group_words(g):
             if not in_range(g):
                 return
-            rows = slice(first_tile * P, last_tile * P)
             for c in range(2):
-                if ("grouped%d" % c, g) not in live:
-                    new("grouped%d" % c, g, [P, GROUP, PACK], BF16, 1, align_bytes=64)
-                engine_copy(
-                    out=live["grouped%d" % c, g][:, rows, :].rearrange("q (n i) t -> q n t i", i=4),
-                    in_=live["mixed%d" % c, g][:, :, rows].rearrange("q t (n i) -> q n t i", i=4),
+                nc.scalar.copy(
+                    out=new("grouped%d" % c, g, [P, GROUP, PACK], BF16, 1, align_bytes=64)[:].rearrange(
+                        "q (n i) t -> q n t i", i=4
+                    ),
+                    in_=live["mixed%d" % c, g][:].rearrange("q t (n i) -> q n t i", i=4),
                 )
 
         def quantise(g):
@@ -245,24 +265,13 @@ def tile_rwkv_attention_pa_t_kernel(
             nc.gpsimd.tensor_tensor(
                 out=new_f32("w2", g, 2)[:], in0=sp_all[:, rows_of(g), :], in1=over_tiles(decay_bc), op=ALU.add
             )
-            nc.gpsimd.tensor_scalar(
-                out=new_f32("one_minus_sb", g, 3)[:],
-                in0=sb_all[:, rows_of(g), :],
-                scalar1=-1.0,
-                scalar2=1.0,
-                op0=ALU.mult,
-                op1=ALU.add,
-            )
 
         def compare(g):
             if not in_range(g):
                 return
-            k, v, w2 = live["k", g], live["v", g], live["w2", g]
+            k, w2 = live["k", g], live["w2", g]
             nc.vector.tensor_tensor(out=new_f32("d2", g, 2)[:], in0=k[:], in1=w2[:], op=ALU.subtract)
             nc.vector.tensor_tensor(out=new_f32("p2", g, 2)[:], in0=k[:], in1=w2[:], op=ALU.max)
-            nc.vector.tensor_tensor(
-                out=new_f32("v_minus_sa", g, 2)[:], in0=v[:], in1=sa_all[:, rows_of(g), :], op=ALU.subtract
-            )
             nc.sync.dma_start(out=p2_rows[:, rows_of(g), :], in_=live["p2", g][:])
             nc.gpsimd.tensor_tensor(
                 out=new_f32("d", g, 2)[:], in0=live["d2", g][:], in1=over_tiles(first_plus_decay), op=ALU.add
@@ -274,27 +283,31 @@ def tile_rwkv_attention_pa_t_kernel(
             d2, d = live["d2", g], live["d", g]
             nc.scalar.activation(out=new_f32("exp_up", g, 2)[:], in_=d2[:], func=ACT.Exp)
             nc.scalar.activation(out=new_f32("exp_down", g, 2)[:], in_=d2[:], func=ACT.Exp, scale=-1.0)
-            nc.scalar.activation(out=new_f32("th", g, 2)[:], in_=d[:], func=ACT.Tanh, scale=0.5)
+            nc.scalar.activation(out=new_f32("ratio", g, 2)[:], in_=d[:], func=ACT.Exp, scale=-1.0)
+
+        def both(tile):
+            return tile[:].rearrange("p j a -> p (j a)").unsqueeze(1).to_broadcast([P, 2, TILES * A])
+
+        def half(pair, which):
+            return pair[:, which].rearrange("p (j a) -> p j a", a=A)
 
         def blend(g):
             if not in_range(g):
                 return
-            sa, sb = sa_all[:, rows_of(g), :], sb_all[:, rows_of(g), :]
-            v, th, up, down = live["v", g], live["th", g], live["exp_up", g], live["exp_down", g]
+            v, ratio, up, down = live["v", g], live["ratio", g], live["exp_up", g], live["exp_down", g]
             stt = nc.vector.scalar_tensor_tensor
-            pull, num, f1_sb = new_f32("pull", g, 1), new_f32("num", g, 1), new_f32("f1_sb", g, 1)
-            f1_sa, f2_v = new_f32("f1_sa", g, 2), new_f32("f2_v", g, 2)
-            den_minus_2, num_den = new_f32("den_minus_2", g, 2), new_f32("num_den", g, LN_BATCH + 1)
+            pulled = new("pulled", g, [P, 2, TILES * A], F32, 2)
+            kept = new("kept", g, [P, 2, TILES * A], F32, 2)
+            num, f2_v = new_f32("num", g, 1), new_f32("f2_v", g, 2)
+            num_den = new_f32("num_den", g, LN_BATCH + 1)
             aa, bb = new_f32("aa", g, 2), new_f32("bb", g, 2)
-            stt(out=den_minus_2[:], in0=th[:], scalar=1.0, in1=live["one_minus_sb", g][:], op0=ALU.subtract, op1=ALU.mult)
-            stt(out=pull[:], in0=th[:], scalar=1.0, in1=live["v_minus_sa", g][:], op0=ALU.subtract, op1=ALU.mult)
+            stt(out=pulled[:], in0=both(ratio), scalar=RATIO_MAX, in1=sab_all[:, g], op0=ALU.min, op1=ALU.mult)
+            stt(out=kept[:], in0=both(down), scalar=1.0, in1=sab_all[:, g], op0=ALU.min, op1=ALU.mult)
+            nc.vector.tensor_tensor(out=num[:], in0=v[:], in1=half(pulled, 0), op=ALU.add)
             stt(out=f2_v[:], in0=up[:], scalar=1.0, in1=v[:], op0=ALU.min, op1=ALU.mult)
-            stt(out=num[:], in0=v[:], scalar=2.0, in1=pull[:], op0=ALU.mult, op1=ALU.add)
-            stt(out=f1_sa[:], in0=down[:], scalar=1.0, in1=sa, op0=ALU.min, op1=ALU.mult)
-            stt(out=f1_sb[:], in0=down[:], scalar=1.0, in1=sb, op0=ALU.min, op1=ALU.mult)
-            stt(out=num_den[:], in0=den_minus_2[:], scalar=2.0, in1=num[:], op0=ALU.add, op1=ALU.mult)
-            stt(out=bb[:], in0=up[:], scalar=1.0, in1=f1_sb[:], op0=ALU.min, op1=ALU.add)
-            nc.gpsimd.tensor_tensor(out=aa[:], in0=f1_sa[:], in1=f2_v[:], op=ALU.add)
+            stt(out=bb[:], in0=up[:], scalar=1.0, in1=half(kept, 1), op0=ALU.min, op1=ALU.add)
+            stt(out=num_den[:], in0=half(pulled, 1), scalar=1.0, in1=num[:], op0=ALU.add, op1=ALU.mult)
+            nc.gpsimd.tensor_tensor(out=aa[:], in0=half(kept, 0), in1=f2_v[:], op=ALU.add)
             nc.sync.dma_start(out=aa_rows[:, rows_of(g), :], in_=aa[:])
             nc.sync.dma_start(out=bb_rows[:, rows_of(g), :], in_=bb[:])
 
@@ -302,7 +315,7 @@ def tile_rwkv_attention_pa_t_kernel(
             if not in_range(g):
                 return
             nc.scalar.activation(
-                out=new_f32("inv_den2", g, LN_BATCH)[:], in_=live["den_minus_2", g][:], func=ACT.Square, bias=two[:, 0:1]
+                out=new_f32("inv_den2", g, LN_BATCH)[:], in_=half(live["pulled", g], 1), func=ACT.Square, bias=one[:, 0:1]
             )
 
         def batch_ending_at(g):
@@ -324,16 +337,19 @@ def tile_rwkv_attention_pa_t_kernel(
 
         for i in range(-2, GROUPS + 4):
             load(i + 2)
-            scale_saved_x(i)
-            transpose("sx", i + 1)
-            group_words(i - 1, nc.vector.tensor_copy, 0, VECTOR_TILES)
+            scale_on_scalar(i)
+            transpose("sx", i + 1, 1)
+            transpose("sx", i + 1, 0)
             blend(i - 3)
             compare(i - 2)
             divide(i - 4)
             prepare_state(i - 1)
             mix_x(i)
-            transpose("x", i + 1)
-            group_words(i - 1, nc.scalar.copy, VECTOR_TILES, TILES)
+            transpose("x", i + 1, 0)
+            transpose("x", i + 1, 1)
+            group_words(i - 1)
+            fetch_words(i + 1)
+            scale_on_gpsimd(i + 1)
             quantise(i - 1)
             project(i - 1)
             square_den(i - 3)

@@ -291,31 +291,46 @@ def tile_rwkv_attention_pa_t_kernel(
         def half(pair, which):
             return pair[:, which].rearrange("p (j a) -> p j a", a=A)
 
-        def blend(g):
+        stt = nc.vector.scalar_tensor_tensor
+
+        def scale_state(g):
             if not in_range(g):
                 return
-            v, ratio, up, down = live["v", g], live["ratio", g], live["exp_up", g], live["exp_down", g]
-            stt = nc.vector.scalar_tensor_tensor
-            pulled = new("pulled", g, [P, 2, TILES * A], F32, 2)
+            ratio, up, down = live["ratio", g], live["exp_up", g], live["exp_down", g]
             kept = new("kept", g, [P, 2, TILES * A], F32, 2)
-            num, f2_v = new_f32("num", g, 1), new_f32("f2_v", g, 2)
-            num_den = new_f32("num_den", g, LN_BATCH + 1)
-            aa, bb = new_f32("aa", g, 2), new_f32("bb", g, 2)
-            stt(out=pulled[:], in0=both(ratio), scalar=RATIO_MAX, in1=sab_all[:, g], op0=ALU.min, op1=ALU.mult)
+            pulled = new("pulled", g, [P, 2, TILES * A], F32, 2)
+            bb = new_f32("bb", g, 2)
             stt(out=kept[:], in0=both(down), scalar=1.0, in1=sab_all[:, g], op0=ALU.min, op1=ALU.mult)
-            nc.vector.tensor_tensor(out=num[:], in0=v[:], in1=half(pulled, 0), op=ALU.add)
-            stt(out=f2_v[:], in0=up[:], scalar=1.0, in1=v[:], op0=ALU.min, op1=ALU.mult)
+            stt(out=pulled[:], in0=both(ratio), scalar=RATIO_MAX, in1=sab_all[:, g], op0=ALU.min, op1=ALU.mult)
             stt(out=bb[:], in0=up[:], scalar=1.0, in1=half(kept, 1), op0=ALU.min, op1=ALU.add)
-            stt(out=num_den[:], in0=half(pulled, 1), scalar=1.0, in1=num[:], op0=ALU.add, op1=ALU.mult)
-            nc.gpsimd.tensor_tensor(out=aa[:], in0=half(kept, 0), in1=f2_v[:], op=ALU.add)
-            nc.sync.dma_start(out=aa_rows[:, rows_of(g), :], in_=aa[:])
             nc.sync.dma_start(out=bb_rows[:, rows_of(g), :], in_=bb[:])
+
+        def multiply_num_den(g):
+            if not in_range(g):
+                return
+            stt(
+                out=new_f32("num_den", g, LN_BATCH + 2)[:],
+                in0=half(live["pulled", g], 1),
+                scalar=1.0,
+                in1=live["num", g][:],
+                op0=ALU.add,
+                op1=ALU.mult,
+            )
+
+        def add_v(g):
+            if not in_range(g):
+                return
+            v, f2_v, aa = live["v", g], new_f32("f2_v", g, 2), new_f32("aa", g, 2)
+            stt(out=f2_v[:], in0=live["exp_up", g][:], scalar=1.0, in1=v[:], op0=ALU.min, op1=ALU.mult)
+            nc.vector.tensor_tensor(out=new_f32("num", g, 2)[:], in0=v[:], in1=half(live["pulled", g], 0), op=ALU.add)
+            nc.gpsimd.tensor_tensor(out=aa[:], in0=half(live["kept", g], 0), in1=f2_v[:], op=ALU.add)
+            nc.sync.dma_start(out=aa_rows[:, rows_of(g), :], in_=aa[:])
 
         def square_den(g):
             if not in_range(g):
                 return
             nc.scalar.activation(
-                out=new_f32("inv_den2", g, LN_BATCH)[:], in_=half(live["pulled", g], 1), func=ACT.Square, bias=one[:, 0:1]
+                out=new_f32("inv_den2", g, LN_BATCH + 2)[:], in_=half(live["pulled", g], 1), func=ACT.Square, bias=one[:, 0:1]
             )
 
         def batch_ending_at(g):
@@ -329,20 +344,21 @@ def tile_rwkv_attention_pa_t_kernel(
             for g in batch_ending_at(last):
                 nc.scalar.activation(out=live["inv_den2", g][:], in_=live["inv_den2", g][:], func=ACT.Exp, scale=-1.0)
 
-        def divide(last):
-            for g in batch_ending_at(last):
-                wkv = new_f32("wkv", g, 3)
-                nc.gpsimd.tensor_tensor(out=wkv[:], in0=live["num_den", g][:], in1=live["inv_den2", g][:], op=ALU.mult)
-                nc.sync.dma_start(out=wkv_rows[:, rows_of(g), :], in_=wkv[:])
+        def divide(g, engine):
+            product = live["num_den", g]
+            engine.tensor_tensor(out=product[:], in0=product[:], in1=live["inv_den2", g][:], op=ALU.mult)
+            nc.sync.dma_start(out=wkv_rows[:, rows_of(g), :], in_=product[:])
 
+        inverted = []
         for i in range(-2, GROUPS + 4):
             load(i + 2)
             scale_on_scalar(i)
             transpose("sx", i + 1, 1)
             transpose("sx", i + 1, 0)
-            blend(i - 3)
+            scale_state(i - 3)
+            multiply_num_den(i - 4)
+            add_v(i - 3)
             compare(i - 2)
-            divide(i - 4)
             prepare_state(i - 1)
             mix_x(i)
             transpose("x", i + 1, 0)
@@ -350,6 +366,11 @@ def tile_rwkv_attention_pa_t_kernel(
             group_words(i - 1)
             fetch_words(i + 1)
             scale_on_gpsimd(i + 1)
+            inverted.extend(batch_ending_at(i - 4))
+            last_step = i == GROUPS + 3
+            for g in inverted[: None if last_step else 1 if i < GROUPS else 3]:
+                divide(g, nc.vector if last_step else nc.gpsimd)
+                inverted.remove(g)
             quantise(i - 1)
             project(i - 1)
             square_den(i - 3)

@@ -66,62 +66,62 @@ def tile_rwkv_attention_pa_t_kernel(
         psum = stack.enter_context(tc.psum_pool(name="psum", bufs=1))
         stack.enter_context(tc.manual_schedule())
 
-        identity = const.tile([P, P], F32, name="identity")
-        make_identity(nc, identity[:])
+        one = const.tile([P, 1], F32, name="one")
+        nc.vector.memset(one[:], 1.0)
+        table_loader = const.tile([P, 1], F32, name="table_loader")
+        nc.scalar.activation(out=table_loader[:], in_=one[:], func=ACT.Exp)
 
-        mix_rows = const.tile([P, D], BF16, name="mix_rows")
-        nc.vector.memset(mix_rows[:], 0.0)
-        nc.scalar.dma_start(out=mix_rows[0:1, :], in_=k_mixed.unsqueeze(0))
-        nc.scalar.dma_start(out=mix_rows[1:2, :], in_=v_mixed.unsqueeze(0))
-
-        w_raw = const.tile([P, 2, PACK, A], BF16, name="w_raw")
-        for c, weight in enumerate((key_weight, value_weight)):
-            nc.scalar.dma_start(
-                out=w_raw[:, c], in_=weight.rearrange("(q t) a -> q t a", t=PACK)
-            )
-        decay_bc = const.tile([P, A], BF16, name="decay_bc")
-        first_bc = const.tile([P, A], BF16, name="first_bc")
-        nc.scalar.dma_start(out=decay_bc[:], in_=time_decay.partition_broadcast(P))
-        nc.scalar.dma_start(out=first_bc[:], in_=time_first.partition_broadcast(P))
-
-        mix_t = psum.tile([P, GROUP], F32, name="mix_t", tag="x_t0")
-        for u in range(HALVES):
-            nc.tensor.transpose(
-                out=mix_t[:, u * P : (u + 1) * P],
-                in_=mix_rows[:].bitcast(F32)[:, u::HALVES],
-                identity=identity[:],
-            )
+        mix_bf16 = const.tile([P, 2, 16], BF16, name="mix_bf16")
+        for c, vector in enumerate((k_mixed, v_mixed)):
+            nc.sync.dma_start(out=mix_bf16[:, c, 0:PACK], in_=vector.rearrange("(q t) -> q t", t=PACK))
         mix = const.tile([P, 2, PACK], F32, name="mix")
-        for u in range(HALVES):
-            first_column = u * P * PAIR
-            nc.vector.tensor_copy(
-                out=mix[:, :, PAIR * u : PAIR * (u + 1)],
-                in_=mix_t[:]
-                .bitcast(BF16)[:, first_column : first_column + 2 * PAIR]
-                .rearrange("q (c e) -> q c e", e=PAIR),
-            )
+        nc.vector.tensor_copy(out=mix[:], in_=mix_bf16[:, :, 0:PACK])
         one_minus_mix = const.tile([P, 2, PACK], F32, name="one_minus_mix")
         nc.vector.tensor_scalar(
             out=one_minus_mix[:], in0=mix[:], scalar1=-1.0, scalar2=1.0, op0=ALU.mult, op1=ALU.add
         )
 
+        identity = const.tile([P, P], F32, name="identity")
+        make_identity(nc, identity[:])
+
+        state_rows = const.tile([P, 2, A], BF16, name="state_rows")
+        nc.gpsimd.memset(state_rows[:], 0.0)
+        nc.scalar.dma_start(out=state_rows[0:1, 0, :], in_=time_decay.unsqueeze(0))
+        nc.scalar.dma_start(out=state_rows[0:1, 1, :], in_=time_first.unsqueeze(0))
+        ones = const.tile([P, P], BF16, name="ones")
+        nc.gpsimd.memset(ones[:], 1.0)
+
+        w_raw = const.tile([P, 2, PACK, A], BF16, name="w_raw")
         w_grouped = const.tile([P, 2, A, PACK], BF16, name="w_grouped", align_bytes=64)
-        for c in range(2):
-            nc.vector.tensor_copy(out=w_grouped[:, c], in_=w_raw[:, c].rearrange("q t a -> q a t"))
         w_codes = const.tile([P, 2 * A], U32, name="w_codes", align_bytes=64)
         w_scales = const.tile([P, 2 * A], U8, name="w_scales", align_bytes=64)
-        nc.vector.quantize_mx(
-            out=w_codes[:].bitcast(FP8X4),
-            scales=w_scales[:],
-            in_=w_grouped[:].rearrange("q c a t -> q (c a t)"),
-        )
-
+        decay_bc = const.tile([P, A], F32, name="decay_bc")
         first_plus_decay = const.tile([P, A], F32, name="first_plus_decay")
-        nc.vector.tensor_tensor(
-            out=first_plus_decay[:], in0=first_bc[:], in1=decay_bc[:], op=ALU.add
-        )
-        one = const.tile([P, 1], F32, name="one")
-        nc.vector.memset(one[:], 1.0)
+
+        def load_weights():
+            for c, weight in enumerate((key_weight, value_weight)):
+                nc.sync.dma_start(out=w_raw[:, c], in_=weight.rearrange("(q t) a -> q t a", t=PACK))
+
+        def spread_state_rows():
+            spread = psum.tile([P, 2, A], F32, name="spread", tag="k")
+            nc.tensor.matmul(
+                out=spread[:].rearrange("p v a -> p (v a)"),
+                lhsT=ones[:],
+                rhs=state_rows[:].rearrange("p v a -> p (v a)"),
+                start=True,
+                stop=True,
+            )
+            nc.vector.tensor_copy(out=decay_bc[:], in_=spread[:, 0, :])
+            nc.vector.tensor_tensor(out=first_plus_decay[:], in0=spread[:, 1, :], in1=decay_bc[:], op=ALU.add)
+
+        def quantise_weights():
+            for c in range(2):
+                nc.vector.tensor_copy(out=w_grouped[:, c], in_=w_raw[:, c].rearrange("q t a -> q a t"))
+            nc.vector.quantize_mx(
+                out=w_codes[:].bitcast(FP8X4),
+                scales=w_scales[:],
+                in_=w_grouped[:].rearrange("q c a t -> q (c a t)"),
+            )
 
         def over_tiles(row):
             return row[:].unsqueeze(1).to_broadcast([P, TILES, A])
@@ -352,6 +352,8 @@ def tile_rwkv_attention_pa_t_kernel(
         inverted = []
         for i in range(-2, GROUPS + 4):
             load(i + 2)
+            if i == -2:
+                load_weights()
             scale_on_scalar(i)
             transpose("sx", i + 1, 1)
             transpose("sx", i + 1, 0)
@@ -361,6 +363,9 @@ def tile_rwkv_attention_pa_t_kernel(
             compare(i - 2)
             prepare_state(i - 1)
             mix_x(i)
+            if i == 0:
+                spread_state_rows()
+                quantise_weights()
             transpose("x", i + 1, 0)
             transpose("x", i + 1, 1)
             group_words(i - 1)

@@ -21,7 +21,8 @@ TILES = 4
 GROUP = TILES * P
 GROUPS = B // GROUP
 RATIO_MAX = 2.0**32
-LN_BATCH = 5
+STATES_PER_STEP = 3
+LN_ENDS = (4, 9, 11)
 
 FLOPS = 2 * 2 * B * D * A
 
@@ -96,7 +97,7 @@ def tile_rwkv_attention_pa_t_kernel(
         w_codes = const.tile([P, 2 * A], U32, name="w_codes", align_bytes=64)
         w_scales = const.tile([P, 2 * A], U8, name="w_scales", align_bytes=64)
         decay_bc = const.tile([P, A], F32, name="decay_bc")
-        first_plus_decay = const.tile([P, A], F32, name="first_plus_decay")
+        column_ratio = const.tile([P, A], F32, name="column_ratio")
 
         def load_weights():
             for c, weight in enumerate((key_weight, value_weight)):
@@ -112,7 +113,8 @@ def tile_rwkv_attention_pa_t_kernel(
                 stop=True,
             )
             nc.vector.tensor_copy(out=decay_bc[:], in_=spread[:, 0, :])
-            nc.vector.tensor_tensor(out=first_plus_decay[:], in0=spread[:, 1, :], in1=decay_bc[:], op=ALU.add)
+            nc.vector.tensor_tensor(out=column_ratio[:], in0=spread[:, 1, :], in1=decay_bc[:], op=ALU.add)
+            nc.scalar.activation(out=column_ratio[:], in_=column_ratio[:], func=ACT.Exp, scale=-1.0)
 
         def quantise_weights():
             for c in range(2):
@@ -145,11 +147,17 @@ def tile_rwkv_attention_pa_t_kernel(
                 return
             nc.sync.dma_start(out=new("sx", g, [P, TILES, D], BF16, 3)[:], in_=sx_rows[:, rows_of(g), :])
             nc.sync.dma_start(out=new("x", g, [P, TILES, D], BF16, 3)[:], in_=x_rows[:, rows_of(g), :])
-            nc.sync.dma_start(out=sp_all[:, rows_of(g), :], in_=sp_rows[:, rows_of(g), :])
             for which, rows in enumerate((sa_rows, sb_rows)):
                 nc.sync.dma_start(
                     out=sab_all[:, g, which].rearrange("p (j a) -> p j a", a=A), in_=rows[:, rows_of(g), :]
                 )
+
+        def states_of_step(i):
+            return range(STATES_PER_STEP * (i - 1), min(STATES_PER_STEP * i, GROUPS)) if i > 0 else ()
+
+        def load_states(i):
+            for g in states_of_step(i):
+                nc.sync.dma_start(out=sp_all[:, rows_of(g), :], in_=sp_rows[:, rows_of(g), :])
 
         def transpose(name, g, u):
             if not in_range(g):
@@ -170,36 +178,41 @@ def tile_rwkv_attention_pa_t_kernel(
             if not in_range(g):
                 return
             for c in range(2):
-                new("scaled%d0" % c, g, [P, PAIR, GROUP], F32, 2)
+                new("scaled%d" % c, g, [P, PAIR, GROUP], F32, 2)
             for e in range(PAIR):
                 for c in range(2):
                     nc.scalar.activation(
-                        out=live["scaled%d0" % c, g][:, e, :],
-                        in_=value_of_word(live["sx_t0", g], e),
+                        out=live["scaled%d" % c, g][:, e, :],
+                        in_=value_of_word(live["sx_t1", g], e),
                         func=ACT.Copy,
-                        scale=one_minus_mix[:, c, e : e + 1],
+                        scale=one_minus_mix[:, c, PAIR + e : PAIR + e + 1],
                     )
 
         def fetch_words(g):
             if not in_range(g):
                 return
-            nc.scalar.copy(out=new("sx_words", g, [P, GROUP], F32, 2)[:], in_=live["sx_t1", g][:])
+            nc.scalar.copy(out=new("sx_words", g, [P, GROUP], F32, 2)[:], in_=live["sx_t0", g][:])
 
-        def scale_on_gpsimd(g):
+        def subtract_rows(g):
             if not in_range(g):
                 return
-            for c in range(2):
-                new("scaled%d1" % c, g, [P, PAIR, GROUP], F32, 2)
-            for e in range(PAIR):
-                for c in range(2):
-                    t = PAIR + e
-                    nc.gpsimd.tensor_scalar(
-                        out=live["scaled%d1" % c, g][:, e, :],
-                        in0=value_of_word(live["sx_words", g], e),
-                        scalar1=one_minus_mix[:, c, t : t + 1],
-                        scalar2=0.0,
-                        op0=ALU.mult,
-                        op1=ALU.add,
+            difference = new("difference", g, [P, PAIR, TILES, P], F32, 2)
+            for t in range(PAIR):
+                nc.gpsimd.tensor_tensor(
+                    out=difference[:, t],
+                    in0=live["x", g][:, :, t::PACK],
+                    in1=live["sx", g][:, :, t::PACK],
+                    op=ALU.subtract,
+                )
+
+        def transpose_difference(g):
+            if not in_range(g):
+                return
+            for t in range(PAIR):
+                bank = new("difference_t%d" % t, g, [P, GROUP], F32, 1, pool=psum)
+                for j in range(TILES):
+                    nc.tensor.transpose(
+                        out=bank[:, j * P : (j + 1) * P], in_=live["difference", g][:, t, j], identity=identity[:]
                     )
 
         def mix_x(g):
@@ -207,28 +220,27 @@ def tile_rwkv_attention_pa_t_kernel(
                 return
             for c in range(2):
                 new("mixed%d" % c, g, [P, PACK, GROUP], BF16, 2)
-            for t in range(PACK):
+            for t in (2, 3, 0, 1):
                 u, e = divmod(t, PAIR)
                 for c in range(2):
                     nc.vector.scalar_tensor_tensor(
                         out=live["mixed%d" % c, g][:, t, :],
-                        in0=value_of_word(live["x_t%d" % u, g], e),
+                        in0=value_of_word(live["x_t1", g], e) if u else live["difference_t%d" % t, g][:],
                         scalar=mix[:, c, t : t + 1],
-                        in1=live["scaled%d%d" % (c, u), g][:, e, :],
+                        in1=live["scaled%d" % c, g][:, e, :] if u else value_of_word(live["sx_words", g], e),
                         op0=ALU.mult,
                         op1=ALU.add,
                     )
 
-        def group_words(g):
+        def group_words(g, c):
             if not in_range(g):
                 return
-            for c in range(2):
-                nc.scalar.copy(
-                    out=new("grouped%d" % c, g, [P, GROUP, PACK], BF16, 1, align_bytes=64)[:].rearrange(
-                        "q (n i) t -> q n t i", i=4
-                    ),
-                    in_=live["mixed%d" % c, g][:].rearrange("q t (n i) -> q n t i", i=4),
-                )
+            nc.scalar.copy(
+                out=new("grouped%d" % c, g, [P, GROUP, PACK], BF16, 1, align_bytes=64)[:].rearrange(
+                    "q (n i) t -> q n t i", i=4
+                ),
+                in_=live["mixed%d" % c, g][:].rearrange("q t (n i) -> q n t i", i=4),
+            )
 
         def quantise(g):
             if not in_range(g):
@@ -263,7 +275,7 @@ def tile_rwkv_attention_pa_t_kernel(
             if not in_range(g):
                 return
             nc.gpsimd.tensor_tensor(
-                out=new_f32("w2", g, 2)[:], in0=sp_all[:, rows_of(g), :], in1=over_tiles(decay_bc), op=ALU.add
+                out=new_f32("w2", g, 8)[:], in0=sp_all[:, rows_of(g), :], in1=over_tiles(decay_bc), op=ALU.add
             )
 
         def compare(g):
@@ -273,17 +285,18 @@ def tile_rwkv_attention_pa_t_kernel(
             nc.vector.tensor_tensor(out=new_f32("d2", g, 2)[:], in0=k[:], in1=w2[:], op=ALU.subtract)
             nc.vector.tensor_tensor(out=new_f32("p2", g, 2)[:], in0=k[:], in1=w2[:], op=ALU.max)
             nc.sync.dma_start(out=p2_rows[:, rows_of(g), :], in_=live["p2", g][:])
-            nc.gpsimd.tensor_tensor(
-                out=new_f32("d", g, 2)[:], in0=live["d2", g][:], in1=over_tiles(first_plus_decay), op=ALU.add
-            )
 
         def exponentials(g):
             if not in_range(g):
                 return
-            d2, d = live["d2", g], live["d", g]
+            d2 = live["d2", g]
             nc.scalar.activation(out=new_f32("exp_up", g, 2)[:], in_=d2[:], func=ACT.Exp)
-            nc.scalar.activation(out=new_f32("exp_down", g, 2)[:], in_=d2[:], func=ACT.Exp, scale=-1.0)
-            nc.scalar.activation(out=new_f32("ratio", g, 2)[:], in_=d[:], func=ACT.Exp, scale=-1.0)
+            down = new_f32("exp_down", g, 2)
+            nc.scalar.activation(out=down[:], in_=d2[:], func=ACT.Exp, scale=-1.0)
+            engine = nc.vector if g >= GROUPS - 1 else nc.gpsimd
+            engine.tensor_tensor(
+                out=new_f32("ratio", g, 2)[:], in0=down[:], in1=over_tiles(column_ratio), op=ALU.mult
+            )
 
         def both(tile):
             return tile[:].rearrange("p j a -> p (j a)").unsqueeze(1).to_broadcast([P, 2, TILES * A])
@@ -309,7 +322,7 @@ def tile_rwkv_attention_pa_t_kernel(
             if not in_range(g):
                 return
             stt(
-                out=new_f32("num_den", g, LN_BATCH + 2)[:],
+                out=new_f32("num_den", g, 7)[:],
                 in0=half(live["pulled", g], 1),
                 scalar=1.0,
                 in1=live["num", g][:],
@@ -323,25 +336,23 @@ def tile_rwkv_attention_pa_t_kernel(
             v, f2_v, aa = live["v", g], new_f32("f2_v", g, 2), new_f32("aa", g, 2)
             stt(out=f2_v[:], in0=live["exp_up", g][:], scalar=1.0, in1=v[:], op0=ALU.min, op1=ALU.mult)
             nc.vector.tensor_tensor(out=new_f32("num", g, 2)[:], in0=v[:], in1=half(live["pulled", g], 0), op=ALU.add)
-            nc.gpsimd.tensor_tensor(out=aa[:], in0=half(live["kept", g], 0), in1=f2_v[:], op=ALU.add)
+            engine = nc.vector if g >= GROUPS - 2 else nc.gpsimd
+            engine.tensor_tensor(out=aa[:], in0=half(live["kept", g], 0), in1=f2_v[:], op=ALU.add)
             nc.sync.dma_start(out=aa_rows[:, rows_of(g), :], in_=aa[:])
 
         def square_den(g):
             if not in_range(g):
                 return
             nc.scalar.activation(
-                out=new_f32("inv_den2", g, LN_BATCH + 2)[:], in_=half(live["pulled", g], 1), func=ACT.Square, bias=one[:, 0:1]
+                out=new_f32("inv_den2", g, 7)[:], in_=half(live["pulled", g], 1), func=ACT.Square, bias=one[:, 0:1]
             )
 
-        def batch_ending_at(g):
-            if in_range(g) and ((g + 1) % LN_BATCH == 0 or g == GROUPS - 1):
-                return range(g // LN_BATCH * LN_BATCH, g + 1)
-            return range(0)
-
-        def invert_den2(last):
-            for g in batch_ending_at(last):
+        def logarithms(groups):
+            for g in groups:
                 nc.scalar.activation(out=live["inv_den2", g][:], in_=live["inv_den2", g][:], func=ACT.Ln)
-            for g in batch_ending_at(last):
+
+        def inverses(groups):
+            for g in groups:
                 nc.scalar.activation(out=live["inv_den2", g][:], in_=live["inv_den2", g][:], func=ACT.Exp, scale=-1.0)
 
         def divide(g, engine):
@@ -352,32 +363,42 @@ def tile_rwkv_attention_pa_t_kernel(
         inverted = []
         for i in range(-2, GROUPS + 4):
             load(i + 2)
+            load_states(i + 2)
             if i == -2:
                 load_weights()
             scale_on_scalar(i)
-            transpose("sx", i + 1, 1)
             transpose("sx", i + 1, 0)
+            transpose("sx", i + 1, 1)
+            tail = i >= GROUPS
+            if tail:
+                compare(i - 2)
             scale_state(i - 3)
             multiply_num_den(i - 4)
             add_v(i - 3)
-            compare(i - 2)
-            prepare_state(i - 1)
+            if not tail:
+                compare(i - 2)
+            group_words(i - 1, 0)
+            fetch_words(i + 1)
+            subtract_rows(i + 1)
+            exponentials(i - 2)
+            group_words(i - 1, 1)
+            for g in states_of_step(i):
+                prepare_state(g)
             mix_x(i)
             if i == 0:
                 spread_state_rows()
                 quantise_weights()
-            transpose("x", i + 1, 0)
             transpose("x", i + 1, 1)
-            group_words(i - 1)
-            fetch_words(i + 1)
-            scale_on_gpsimd(i + 1)
-            inverted.extend(batch_ending_at(i - 4))
+            transpose_difference(i + 1)
             last_step = i == GROUPS + 3
-            for g in inverted[: None if last_step else 1 if i < GROUPS else 3]:
-                divide(g, nc.vector if last_step else nc.gpsimd)
+            for g in inverted[: None if last_step else 1 if i < GROUPS else 2]:
+                inverses([g])
+                divide(g, nc.vector if last_step and g % 2 else nc.gpsimd)
                 inverted.remove(g)
             quantise(i - 1)
             project(i - 1)
             square_den(i - 3)
-            exponentials(i - 2)
-            invert_den2(i - 3)
+            if i - 3 in LN_ENDS:
+                first = 0 if i - 3 == LN_ENDS[0] else LN_ENDS[LN_ENDS.index(i - 3) - 1] + 1
+                logarithms(range(first, i - 2))
+                inverted.extend(range(first, i - 2))

@@ -21,6 +21,7 @@ TILES = 4
 GROUP = TILES * P
 GROUPS = B // GROUP
 RATIO_MAX = 2.0**32
+VECTOR_ROWS = 96
 STATES_PER_STEP = 3
 LN_ENDS = (4, 9, 11)
 
@@ -114,7 +115,6 @@ def tile_rwkv_attention_pa_t_kernel(
             )
             nc.vector.tensor_copy(out=decay_bc[:], in_=spread[:, 0, :])
             nc.vector.tensor_tensor(out=column_ratio[:], in0=spread[:, 1, :], in1=decay_bc[:], op=ALU.add)
-            nc.scalar.activation(out=column_ratio[:], in_=column_ratio[:], func=ACT.Exp, scale=-1.0)
 
         def quantise_weights():
             for c in range(2):
@@ -174,45 +174,19 @@ def tile_rwkv_attention_pa_t_kernel(
         def value_of_word(bank, e):
             return bank[:].bitcast(BF16).rearrange("q (r e) -> q e r", e=PAIR)[:, e, :]
 
-        def scale_on_scalar(g):
+        def scale_saved_x(g, u):
             if not in_range(g):
                 return
             for c in range(2):
-                new("scaled%d" % c, g, [P, PAIR, GROUP], F32, 2)
+                new("scaled%d%d" % (c, u), g, [P, PAIR, GROUP], F32, 2)
             for e in range(PAIR):
                 for c in range(2):
+                    t = PAIR * u + e
                     nc.scalar.activation(
-                        out=live["scaled%d" % c, g][:, e, :],
-                        in_=value_of_word(live["sx_t1", g], e),
+                        out=live["scaled%d%d" % (c, u), g][:, e, :],
+                        in_=value_of_word(live["sx_t%d" % u, g], e),
                         func=ACT.Copy,
-                        scale=one_minus_mix[:, c, PAIR + e : PAIR + e + 1],
-                    )
-
-        def fetch_words(g):
-            if not in_range(g):
-                return
-            nc.scalar.copy(out=new("sx_words", g, [P, GROUP], F32, 2)[:], in_=live["sx_t0", g][:])
-
-        def subtract_rows(g):
-            if not in_range(g):
-                return
-            difference = new("difference", g, [P, PAIR, TILES, P], F32, 2)
-            for t in range(PAIR):
-                nc.gpsimd.tensor_tensor(
-                    out=difference[:, t],
-                    in0=live["x", g][:, :, t::PACK],
-                    in1=live["sx", g][:, :, t::PACK],
-                    op=ALU.subtract,
-                )
-
-        def transpose_difference(g):
-            if not in_range(g):
-                return
-            for t in range(PAIR):
-                bank = new("difference_t%d" % t, g, [P, GROUP], F32, 1, pool=psum)
-                for j in range(TILES):
-                    nc.tensor.transpose(
-                        out=bank[:, j * P : (j + 1) * P], in_=live["difference", g][:, t, j], identity=identity[:]
+                        scale=one_minus_mix[:, c, t : t + 1],
                     )
 
         def mix_x(g):
@@ -220,26 +194,27 @@ def tile_rwkv_attention_pa_t_kernel(
                 return
             for c in range(2):
                 new("mixed%d" % c, g, [P, PACK, GROUP], BF16, 2)
-            for t in (2, 3, 0, 1):
+            for t in range(PACK):
                 u, e = divmod(t, PAIR)
                 for c in range(2):
                     nc.vector.scalar_tensor_tensor(
                         out=live["mixed%d" % c, g][:, t, :],
-                        in0=value_of_word(live["x_t1", g], e) if u else live["difference_t%d" % t, g][:],
+                        in0=value_of_word(live["x_t%d" % u, g], e),
                         scalar=mix[:, c, t : t + 1],
-                        in1=live["scaled%d" % c, g][:, e, :] if u else value_of_word(live["sx_words", g], e),
+                        in1=live["scaled%d%d" % (c, u), g][:, e, :],
                         op0=ALU.mult,
                         op1=ALU.add,
                     )
 
-        def group_words(g, c):
+        def group_words(g, c, engine_copy, first_row, last_row):
             if not in_range(g):
                 return
-            nc.scalar.copy(
-                out=new("grouped%d" % c, g, [P, GROUP, PACK], BF16, 1, align_bytes=64)[:].rearrange(
-                    "q (n i) t -> q n t i", i=4
-                ),
-                in_=live["mixed%d" % c, g][:].rearrange("q t (n i) -> q n t i", i=4),
+            rows = slice(first_row, last_row)
+            if ("grouped%d" % c, g) not in live:
+                new("grouped%d" % c, g, [P, GROUP, PACK], BF16, 1, align_bytes=64)
+            engine_copy(
+                out=live["grouped%d" % c, g][:, rows, :].rearrange("q (n i) t -> q n t i", i=4),
+                in_=live["mixed%d" % c, g][:, :, rows].rearrange("q t (n i) -> q n t i", i=4),
             )
 
         def quantise(g):
@@ -366,7 +341,8 @@ def tile_rwkv_attention_pa_t_kernel(
             load_states(i + 2)
             if i == -2:
                 load_weights()
-            scale_on_scalar(i)
+            scale_saved_x(i, 0)
+            scale_saved_x(i, 1)
             transpose("sx", i + 1, 0)
             transpose("sx", i + 1, 1)
             tail = i >= GROUPS
@@ -374,22 +350,24 @@ def tile_rwkv_attention_pa_t_kernel(
                 compare(i - 2)
             scale_state(i - 3)
             multiply_num_den(i - 4)
+            for c in range(2):
+                group_words(i - 1, c, nc.vector.tensor_copy, 0, VECTOR_ROWS)
             add_v(i - 3)
             if not tail:
                 compare(i - 2)
-            group_words(i - 1, 0)
-            fetch_words(i + 1)
-            subtract_rows(i + 1)
+            group_words(i - 1, 0, nc.scalar.copy, VECTOR_ROWS, GROUP)
             exponentials(i - 2)
-            group_words(i - 1, 1)
+            group_words(i - 1, 1, nc.scalar.copy, VECTOR_ROWS, GROUP)
+            if i == 1:
+                nc.scalar.activation(out=column_ratio[:], in_=column_ratio[:], func=ACT.Exp, scale=-1.0)
             for g in states_of_step(i):
                 prepare_state(g)
             mix_x(i)
             if i == 0:
                 spread_state_rows()
                 quantise_weights()
+            transpose("x", i + 1, 0)
             transpose("x", i + 1, 1)
-            transpose_difference(i + 1)
             last_step = i == GROUPS + 3
             for g in inverted[: None if last_step else 1 if i < GROUPS else 2]:
                 inverses([g])

@@ -21,9 +21,8 @@ TILES = 4
 GROUP = TILES * P
 GROUPS = B // GROUP
 RATIO_MAX = 2.0**32
-VECTOR_ROWS = 96
-STATES_PER_STEP = 3
-LN_ENDS = (4, 9, 11)
+STATES_PER_STEP = 2
+LN_BATCH = 5
 
 FLOPS = 2 * 2 * B * D * A
 
@@ -206,15 +205,14 @@ def tile_rwkv_attention_pa_t_kernel(
                         op1=ALU.add,
                     )
 
-        def group_words(g, c, engine_copy, first_row, last_row):
+        def group_words(g, c):
             if not in_range(g):
                 return
-            rows = slice(first_row, last_row)
-            if ("grouped%d" % c, g) not in live:
-                new("grouped%d" % c, g, [P, GROUP, PACK], BF16, 1, align_bytes=64)
+            grouped = new("grouped%d" % c, g, [P, GROUP, PACK], BF16, 1, align_bytes=64)
+            engine_copy = nc.vector.tensor_copy if (g, c) in ((0, 1), (LN_BATCH + 2, 0)) else nc.scalar.copy
             engine_copy(
-                out=live["grouped%d" % c, g][:, rows, :].rearrange("q (n i) t -> q n t i", i=4),
-                in_=live["mixed%d" % c, g][:, :, rows].rearrange("q t (n i) -> q n t i", i=4),
+                out=grouped[:].rearrange("q (n i) t -> q n t i", i=4),
+                in_=live["mixed%d" % c, g][:].rearrange("q t (n i) -> q n t i", i=4),
             )
 
         def quantise(g):
@@ -284,13 +282,19 @@ def tile_rwkv_attention_pa_t_kernel(
         def scale_state(g):
             if not in_range(g):
                 return
-            ratio, up, down = live["ratio", g], live["exp_up", g], live["exp_down", g]
             kept = new("kept", g, [P, 2, TILES * A], F32, 2)
             pulled = new("pulled", g, [P, 2, TILES * A], F32, 2)
+            scalings = [(kept, live["exp_down", g], 1.0), (pulled, live["ratio", g], RATIO_MAX)]
+            if g >= GROUPS - 2:
+                scalings.reverse()
+            for scaled, factor, largest in scalings:
+                stt(out=scaled[:], in0=both(factor), scalar=largest, in1=sab_all[:, g], op0=ALU.min, op1=ALU.mult)
+
+        def add_f2(g):
+            if not in_range(g):
+                return
             bb = new_f32("bb", g, 2)
-            stt(out=kept[:], in0=both(down), scalar=1.0, in1=sab_all[:, g], op0=ALU.min, op1=ALU.mult)
-            stt(out=pulled[:], in0=both(ratio), scalar=RATIO_MAX, in1=sab_all[:, g], op0=ALU.min, op1=ALU.mult)
-            stt(out=bb[:], in0=up[:], scalar=1.0, in1=half(kept, 1), op0=ALU.min, op1=ALU.add)
+            stt(out=bb[:], in0=live["exp_up", g][:], scalar=1.0, in1=half(live["kept", g], 1), op0=ALU.min, op1=ALU.add)
             nc.sync.dma_start(out=bb_rows[:, rows_of(g), :], in_=bb[:])
 
         def multiply_num_den(g):
@@ -350,14 +354,13 @@ def tile_rwkv_attention_pa_t_kernel(
                 compare(i - 2)
             scale_state(i - 3)
             multiply_num_den(i - 4)
-            for c in range(2):
-                group_words(i - 1, c, nc.vector.tensor_copy, 0, VECTOR_ROWS)
+            add_f2(i - 3)
             add_v(i - 3)
             if not tail:
                 compare(i - 2)
-            group_words(i - 1, 0, nc.scalar.copy, VECTOR_ROWS, GROUP)
+            group_words(i - 1, 0)
             exponentials(i - 2)
-            group_words(i - 1, 1, nc.scalar.copy, VECTOR_ROWS, GROUP)
+            group_words(i - 1, 1)
             if i == 1:
                 nc.scalar.activation(out=column_ratio[:], in_=column_ratio[:], func=ACT.Exp, scale=-1.0)
             for g in states_of_step(i):
@@ -375,8 +378,13 @@ def tile_rwkv_attention_pa_t_kernel(
                 inverted.remove(g)
             quantise(i - 1)
             project(i - 1)
+            if i - 3 == GROUPS - 1:
+                logarithms([GROUPS - 2])
             square_den(i - 3)
-            if i - 3 in LN_ENDS:
-                first = 0 if i - 3 == LN_ENDS[0] else LN_ENDS[LN_ENDS.index(i - 3) - 1] + 1
-                logarithms(range(first, i - 2))
-                inverted.extend(range(first, i - 2))
+            if i - 3 == GROUPS - 1:
+                logarithms([GROUPS - 1])
+                inverted.extend([GROUPS - 2, GROUPS - 1])
+            elif (i - 2) % LN_BATCH == 0 and 0 < i - 2 < GROUPS:
+                batch = range(i - 2 - LN_BATCH, i - 2)
+                logarithms(batch)
+                inverted.extend(batch)

@@ -20,9 +20,10 @@ ROWS_PER_PARTITION = B // P
 TILES = 4
 GROUP = TILES * P
 GROUPS = B // GROUP
-RATIO_MAX = 2.0**32
 STATES_PER_STEP = 2
+FIRST_PIECES = 2
 LN_BATCH = 5
+VECTOR_HALVES = ((0, 1), (LN_BATCH + 3, 0))
 
 FLOPS = 2 * 2 * B * D * A
 
@@ -87,8 +88,6 @@ def tile_rwkv_attention_pa_t_kernel(
 
         state_rows = const.tile([P, 2, A], BF16, name="state_rows")
         nc.gpsimd.memset(state_rows[:], 0.0)
-        nc.scalar.dma_start(out=state_rows[0:1, 0, :], in_=time_decay.unsqueeze(0))
-        nc.scalar.dma_start(out=state_rows[0:1, 1, :], in_=time_first.unsqueeze(0))
         ones = const.tile([P, P], BF16, name="ones")
         nc.gpsimd.memset(ones[:], 1.0)
 
@@ -99,7 +98,9 @@ def tile_rwkv_attention_pa_t_kernel(
         decay_bc = const.tile([P, A], F32, name="decay_bc")
         column_ratio = const.tile([P, A], F32, name="column_ratio")
 
-        def load_weights():
+        def load_constants():
+            nc.sync.dma_start(out=state_rows[0:1, 0, :], in_=time_decay.unsqueeze(0))
+            nc.sync.dma_start(out=state_rows[0:1, 1, :], in_=time_first.unsqueeze(0))
             for c, weight in enumerate((key_weight, value_weight)):
                 nc.sync.dma_start(out=w_raw[:, c], in_=weight.rearrange("(q t) a -> q t a", t=PACK))
 
@@ -144,8 +145,12 @@ def tile_rwkv_attention_pa_t_kernel(
         def load(g):
             if not in_range(g):
                 return
-            nc.sync.dma_start(out=new("sx", g, [P, TILES, D], BF16, 3)[:], in_=sx_rows[:, rows_of(g), :])
-            nc.sync.dma_start(out=new("x", g, [P, TILES, D], BF16, 3)[:], in_=x_rows[:, rows_of(g), :])
+            pieces = FIRST_PIECES if g == 0 else 1
+            for name, dram in (("sx", sx_rows), ("x", x_rows)):
+                rows = new(name, g, [P, TILES, D], BF16, 3)
+                for piece in range(pieces):
+                    part = slice(piece * TILES // pieces, (piece + 1) * TILES // pieces)
+                    nc.sync.dma_start(out=rows[:, part, :], in_=dram[:, rows_of(g), :][:, part, :])
             for which, rows in enumerate((sa_rows, sb_rows)):
                 nc.sync.dma_start(
                     out=sab_all[:, g, which].rearrange("p (j a) -> p j a", a=A), in_=rows[:, rows_of(g), :]
@@ -205,11 +210,10 @@ def tile_rwkv_attention_pa_t_kernel(
                         op1=ALU.add,
                     )
 
-        def group_words(g, c):
+        def group_words(g, c, engine_copy):
             if not in_range(g):
                 return
             grouped = new("grouped%d" % c, g, [P, GROUP, PACK], BF16, 1, align_bytes=64)
-            engine_copy = nc.vector.tensor_copy if (g, c) in ((0, 1), (LN_BATCH + 2, 0)) else nc.scalar.copy
             engine_copy(
                 out=grouped[:].rearrange("q (n i) t -> q n t i", i=4),
                 in_=live["mixed%d" % c, g][:].rearrange("q t (n i) -> q n t i", i=4),
@@ -263,13 +267,8 @@ def tile_rwkv_attention_pa_t_kernel(
             if not in_range(g):
                 return
             d2 = live["d2", g]
-            nc.scalar.activation(out=new_f32("exp_up", g, 2)[:], in_=d2[:], func=ACT.Exp)
-            down = new_f32("exp_down", g, 2)
-            nc.scalar.activation(out=down[:], in_=d2[:], func=ACT.Exp, scale=-1.0)
-            engine = nc.vector if g >= GROUPS - 1 else nc.gpsimd
-            engine.tensor_tensor(
-                out=new_f32("ratio", g, 2)[:], in0=down[:], in1=over_tiles(column_ratio), op=ALU.mult
-            )
+            nc.scalar.activation(out=new_f32("exp_up", g, 3)[:], in_=d2[:], func=ACT.Exp)
+            nc.scalar.activation(out=new_f32("exp_down", g, 2)[:], in_=d2[:], func=ACT.Exp, scale=-1.0)
 
         def both(tile):
             return tile[:].rearrange("p j a -> p (j a)").unsqueeze(1).to_broadcast([P, 2, TILES * A])
@@ -283,12 +282,17 @@ def tile_rwkv_attention_pa_t_kernel(
             if not in_range(g):
                 return
             kept = new("kept", g, [P, 2, TILES * A], F32, 2)
-            pulled = new("pulled", g, [P, 2, TILES * A], F32, 2)
-            scalings = [(kept, live["exp_down", g], 1.0), (pulled, live["ratio", g], RATIO_MAX)]
-            if g >= GROUPS - 2:
-                scalings.reverse()
-            for scaled, factor, largest in scalings:
-                stt(out=scaled[:], in0=both(factor), scalar=largest, in1=sab_all[:, g], op0=ALU.min, op1=ALU.mult)
+            stt(out=kept[:], in0=both(live["exp_down", g]), scalar=1.0, in1=sab_all[:, g], op0=ALU.min, op1=ALU.mult)
+
+        def weigh_state(g, engine):
+            if not in_range(g):
+                return
+            engine.tensor_tensor(
+                out=new("weighed", g, [P, 2 * TILES, A], F32, 2)[:],
+                in0=live["kept", g][:].rearrange("p w (j a) -> p (w j) a", a=A),
+                in1=column_ratio[:].unsqueeze(1).to_broadcast([P, 2 * TILES, A]),
+                op=ALU.mult,
+            )
 
         def add_f2(g):
             if not in_range(g):
@@ -297,34 +301,46 @@ def tile_rwkv_attention_pa_t_kernel(
             stt(out=bb[:], in0=live["exp_up", g][:], scalar=1.0, in1=half(live["kept", g], 1), op0=ALU.min, op1=ALU.add)
             nc.sync.dma_start(out=bb_rows[:, rows_of(g), :], in_=bb[:])
 
-        def multiply_num_den(g):
-            if not in_range(g):
+        def make_num_and_den(g):
+            if not in_range(g) or ("den", g) in live:
                 return
+            weighed = live["weighed", g]
             stt(
-                out=new_f32("num_den", g, 7)[:],
-                in0=half(live["pulled", g], 1),
+                out=new_f32("den", g, 2)[:],
+                in0=live["exp_up", g][:],
                 scalar=1.0,
-                in1=live["num", g][:],
-                op0=ALU.add,
-                op1=ALU.mult,
+                in1=weighed[:, TILES : 2 * TILES],
+                op0=ALU.min,
+                op1=ALU.add,
+            )
+            nc.vector.tensor_tensor(
+                out=new_f32("num", g, 2)[:], in0=weighed[:, 0:TILES], in1=live["f2_v", g][:], op=ALU.add
             )
 
-        def add_v(g):
+        def multiply_num_den(g):
+            if not in_range(g) or ("num_den", g) in live:
+                return
+            nc.vector.tensor_tensor(
+                out=new_f32("num_den", g, 7)[:], in0=live["num", g][:], in1=live["den", g][:], op=ALU.mult
+            )
+
+        def scale_v(g):
             if not in_range(g):
                 return
-            v, f2_v, aa = live["v", g], new_f32("f2_v", g, 2), new_f32("aa", g, 2)
-            stt(out=f2_v[:], in0=live["exp_up", g][:], scalar=1.0, in1=v[:], op0=ALU.min, op1=ALU.mult)
-            nc.vector.tensor_tensor(out=new_f32("num", g, 2)[:], in0=v[:], in1=half(live["pulled", g], 0), op=ALU.add)
-            engine = nc.vector if g >= GROUPS - 2 else nc.gpsimd
-            engine.tensor_tensor(out=aa[:], in0=half(live["kept", g], 0), in1=f2_v[:], op=ALU.add)
+            f2_v = new_f32("f2_v", g, 3)
+            stt(out=f2_v[:], in0=live["exp_up", g][:], scalar=1.0, in1=live["v", g][:], op0=ALU.min, op1=ALU.mult)
+
+        def add_products(g, engine):
+            if not in_range(g):
+                return
+            aa = new_f32("aa", g, 2)
+            engine.tensor_tensor(out=aa[:], in0=half(live["kept", g], 0), in1=live["f2_v", g][:], op=ALU.add)
             nc.sync.dma_start(out=aa_rows[:, rows_of(g), :], in_=aa[:])
 
         def square_den(g):
-            if not in_range(g):
+            if not in_range(g) or ("inv_den2", g) in live:
                 return
-            nc.scalar.activation(
-                out=new_f32("inv_den2", g, 7)[:], in_=half(live["pulled", g], 1), func=ACT.Square, bias=one[:, 0:1]
-            )
+            nc.scalar.activation(out=new_f32("inv_den2", g, 7)[:], in_=live["den", g][:], func=ACT.Square)
 
         def logarithms(groups):
             for g in groups:
@@ -344,7 +360,7 @@ def tile_rwkv_attention_pa_t_kernel(
             load(i + 2)
             load_states(i + 2)
             if i == -2:
-                load_weights()
+                load_constants()
             scale_saved_x(i, 0)
             scale_saved_x(i, 1)
             transpose("sx", i + 1, 0)
@@ -352,15 +368,28 @@ def tile_rwkv_attention_pa_t_kernel(
             tail = i >= GROUPS
             if tail:
                 compare(i - 2)
+            last_blend = i - 3 == GROUPS - 1
+            make_num_and_den(i - 4)
             scale_state(i - 3)
             multiply_num_den(i - 4)
             add_f2(i - 3)
-            add_v(i - 3)
+            for c in range(2):
+                if (i - 1, c) in VECTOR_HALVES:
+                    group_words(i - 1, c, nc.vector.tensor_copy)
+            helper = nc.gpsimd if i - 3 < GROUPS - 2 else nc.vector
             if not tail:
                 compare(i - 2)
-            group_words(i - 1, 0)
+            scale_v(i - 3)
+            weigh_state(i - 3, helper)
+            add_products(i - 3, helper)
+            if last_blend:
+                make_num_and_den(GROUPS - 1)
+                multiply_num_den(GROUPS - 1)
+            if (i - 1, 0) not in VECTOR_HALVES:
+                group_words(i - 1, 0, nc.scalar.copy)
             exponentials(i - 2)
-            group_words(i - 1, 1)
+            if (i - 1, 1) not in VECTOR_HALVES:
+                group_words(i - 1, 1, nc.scalar.copy)
             if i == 1:
                 nc.scalar.activation(out=column_ratio[:], in_=column_ratio[:], func=ACT.Exp, scale=-1.0)
             for g in states_of_step(i):
@@ -378,13 +407,13 @@ def tile_rwkv_attention_pa_t_kernel(
                 inverted.remove(g)
             quantise(i - 1)
             project(i - 1)
-            if i - 3 == GROUPS - 1:
-                logarithms([GROUPS - 2])
-            square_den(i - 3)
-            if i - 3 == GROUPS - 1:
+            square_den(i - 4)
+            if last_blend:
+                logarithms([GROUPS - 3, GROUPS - 2])
+                square_den(GROUPS - 1)
                 logarithms([GROUPS - 1])
-                inverted.extend([GROUPS - 2, GROUPS - 1])
-            elif (i - 2) % LN_BATCH == 0 and 0 < i - 2 < GROUPS:
-                batch = range(i - 2 - LN_BATCH, i - 2)
-                logarithms(batch)
-                inverted.extend(batch)
+                inverted.extend([GROUPS - 3, GROUPS - 2, GROUPS - 1])
+            for first, end in ((0, LN_BATCH), (LN_BATCH, GROUPS - 3)):
+                if i - 4 == end - 1:
+                    logarithms(range(first, end))
+                    inverted.extend(range(first, end))

@@ -20,9 +20,11 @@ ROWS_PER_PARTITION = B // P
 TILES = 4
 GROUP = TILES * P
 GROUPS = B // GROUP
-STATES_PER_STEP = 2
+STATES_PER_STEP = 4
 FIRST_PIECES = 2
 LN_BATCH = 5
+VECTOR_ROWS = 176
+FIRST_SHARED, LAST_SHARED = 1, 12
 VECTOR_HALVES = ((0, 1), (LN_BATCH + 3, 0))
 
 FLOPS = 2 * 2 * B * D * A
@@ -128,7 +130,6 @@ def tile_rwkv_attention_pa_t_kernel(
         def over_tiles(row):
             return row[:].unsqueeze(1).to_broadcast([P, TILES, A])
 
-        sab_all = const.tile([P, GROUPS, 2, TILES * A], BF16, name="sab_all")
         sp_all = const.tile([P, ROWS_PER_PARTITION, A], BF16, name="sp_all")
 
         live = {}
@@ -151,13 +152,14 @@ def tile_rwkv_attention_pa_t_kernel(
                 for piece in range(pieces):
                     part = slice(piece * TILES // pieces, (piece + 1) * TILES // pieces)
                     nc.sync.dma_start(out=rows[:, part, :], in_=dram[:, rows_of(g), :][:, part, :])
+            sab = new("sab", g, [P, 2, TILES * A], BF16, 6)
             for which, rows in enumerate((sa_rows, sb_rows)):
                 nc.sync.dma_start(
-                    out=sab_all[:, g, which].rearrange("p (j a) -> p j a", a=A), in_=rows[:, rows_of(g), :]
+                    out=sab[:, which].rearrange("p (j a) -> p j a", a=A), in_=rows[:, rows_of(g), :]
                 )
 
         def states_of_step(i):
-            return range(STATES_PER_STEP * (i - 1), min(STATES_PER_STEP * i, GROUPS)) if i > 0 else ()
+            return range(STATES_PER_STEP * i, min(STATES_PER_STEP * (i + 1), GROUPS)) if i >= 0 else ()
 
         def load_states(i):
             for g in states_of_step(i):
@@ -210,13 +212,15 @@ def tile_rwkv_attention_pa_t_kernel(
                         op1=ALU.add,
                     )
 
-        def group_words(g, c, engine_copy):
+        def group_words(g, c, engine_copy, first_row=0, last_row=GROUP):
             if not in_range(g):
                 return
-            grouped = new("grouped%d" % c, g, [P, GROUP, PACK], BF16, 1, align_bytes=64)
+            if ("grouped%d" % c, g) not in live:
+                new("grouped%d" % c, g, [P, GROUP, PACK], BF16, 1, align_bytes=64)
+            rows = slice(first_row, last_row)
             engine_copy(
-                out=grouped[:].rearrange("q (n i) t -> q n t i", i=4),
-                in_=live["mixed%d" % c, g][:].rearrange("q t (n i) -> q n t i", i=4),
+                out=live["grouped%d" % c, g][:, rows, :].rearrange("q (n i) t -> q n t i", i=4),
+                in_=live["mixed%d" % c, g][:, :, rows].rearrange("q t (n i) -> q n t i", i=4),
             )
 
         def quantise(g):
@@ -252,7 +256,7 @@ def tile_rwkv_attention_pa_t_kernel(
             if not in_range(g):
                 return
             nc.gpsimd.tensor_tensor(
-                out=new_f32("w2", g, 8)[:], in0=sp_all[:, rows_of(g), :], in1=over_tiles(decay_bc), op=ALU.add
+                out=new_f32("w2", g, 12)[:], in0=sp_all[:, rows_of(g), :], in1=over_tiles(decay_bc), op=ALU.add
             )
 
         def compare(g):
@@ -281,66 +285,61 @@ def tile_rwkv_attention_pa_t_kernel(
         def scale_state(g):
             if not in_range(g):
                 return
-            kept = new("kept", g, [P, 2, TILES * A], F32, 2)
-            stt(out=kept[:], in0=both(live["exp_down", g]), scalar=1.0, in1=sab_all[:, g], op0=ALU.min, op1=ALU.mult)
+            state = new("state", g, [P, 4, TILES * A], F32, 3)
+            stt(
+                out=state[:, 0:2], in0=both(live["exp_down", g]), scalar=1.0, in1=live["sab", g][:], op0=ALU.min, op1=ALU.mult
+            )
 
         def weigh_state(g, engine):
             if not in_range(g):
                 return
+
+            def by_tile(parts):
+                return live["state", g][:, parts].rearrange("p w (j a) -> p (w j) a", a=A)
+
             engine.tensor_tensor(
-                out=new("weighed", g, [P, 2 * TILES, A], F32, 2)[:],
-                in0=live["kept", g][:].rearrange("p w (j a) -> p (w j) a", a=A),
+                out=by_tile(slice(2, 4)),
+                in0=by_tile(slice(0, 2)),
                 in1=column_ratio[:].unsqueeze(1).to_broadcast([P, 2 * TILES, A]),
                 op=ALU.mult,
-            )
-
-        def add_f2(g):
-            if not in_range(g):
-                return
-            bb = new_f32("bb", g, 2)
-            stt(out=bb[:], in0=live["exp_up", g][:], scalar=1.0, in1=half(live["kept", g], 1), op0=ALU.min, op1=ALU.add)
-            nc.sync.dma_start(out=bb_rows[:, rows_of(g), :], in_=bb[:])
-
-        def make_num_and_den(g):
-            if not in_range(g) or ("den", g) in live:
-                return
-            weighed = live["weighed", g]
-            stt(
-                out=new_f32("den", g, 2)[:],
-                in0=live["exp_up", g][:],
-                scalar=1.0,
-                in1=weighed[:, TILES : 2 * TILES],
-                op0=ALU.min,
-                op1=ALU.add,
-            )
-            nc.vector.tensor_tensor(
-                out=new_f32("num", g, 2)[:], in0=weighed[:, 0:TILES], in1=live["f2_v", g][:], op=ALU.add
-            )
-
-        def multiply_num_den(g):
-            if not in_range(g) or ("num_den", g) in live:
-                return
-            nc.vector.tensor_tensor(
-                out=new_f32("num_den", g, 7)[:], in0=live["num", g][:], in1=live["den", g][:], op=ALU.mult
             )
 
         def scale_v(g):
             if not in_range(g):
                 return
-            f2_v = new_f32("f2_v", g, 3)
+            f2_v = new_f32("f2_v", g, 2)
             stt(out=f2_v[:], in0=live["exp_up", g][:], scalar=1.0, in1=live["v", g][:], op0=ALU.min, op1=ALU.mult)
 
-        def add_products(g, engine):
+        def add_f2_v(g, engine):
             if not in_range(g):
                 return
-            aa = new_f32("aa", g, 2)
-            engine.tensor_tensor(out=aa[:], in0=half(live["kept", g], 0), in1=live["f2_v", g][:], op=ALU.add)
-            nc.sync.dma_start(out=aa_rows[:, rows_of(g), :], in_=aa[:])
+            aa_num = new("aa_num", g, [P, 2, TILES * A], F32, 2)
+            engine.tensor_tensor(out=aa_num[:], in0=live["state", g][:, 0::2], in1=both(live["f2_v", g]), op=ALU.add)
+            nc.sync.dma_start(out=aa_rows[:, rows_of(g), :], in_=half(aa_num, 0))
+
+        def add_f2(g):
+            if not in_range(g) or ("bb_den", g) in live:
+                return
+            bb_den = new("bb_den", g, [P, 2, TILES * A], F32, 2)
+            stt(
+                out=bb_den[:], in0=both(live["exp_up", g]), scalar=1.0, in1=live["state", g][:, 1::2], op0=ALU.min, op1=ALU.add
+            )
+            nc.sync.dma_start(out=bb_rows[:, rows_of(g), :], in_=half(bb_den, 0))
+
+        def multiply_num_den(g, engine):
+            if not in_range(g) or ("num_den", g) in live:
+                return
+            engine.tensor_tensor(
+                out=new_f32("num_den", g, 7)[:],
+                in0=half(live["aa_num", g], 1),
+                in1=half(live["bb_den", g], 1),
+                op=ALU.mult,
+            )
 
         def square_den(g):
             if not in_range(g) or ("inv_den2", g) in live:
                 return
-            nc.scalar.activation(out=new_f32("inv_den2", g, 7)[:], in_=live["den", g][:], func=ACT.Square)
+            nc.scalar.activation(out=new_f32("inv_den2", g, 7)[:], in_=half(live["bb_den", g], 1), func=ACT.Square)
 
         def logarithms(groups):
             for g in groups:
@@ -369,41 +368,49 @@ def tile_rwkv_attention_pa_t_kernel(
             if tail:
                 compare(i - 2)
             last_blend = i - 3 == GROUPS - 1
-            make_num_and_den(i - 4)
-            scale_state(i - 3)
-            multiply_num_den(i - 4)
-            add_f2(i - 3)
+            add_f2(i - 4)
             for c in range(2):
                 if (i - 1, c) in VECTOR_HALVES:
                     group_words(i - 1, c, nc.vector.tensor_copy)
+                elif c == 0 and i - 1 in range(FIRST_SHARED, LAST_SHARED):
+                    group_words(i - 1, c, nc.vector.tensor_copy, 0, VECTOR_ROWS)
+            scale_state(i - 3)
+            if i - 4 >= LN_BATCH:
+                multiply_num_den(i - 4, nc.vector)
             helper = nc.gpsimd if i - 3 < GROUPS - 2 else nc.vector
             if not tail:
                 compare(i - 2)
-            scale_v(i - 3)
-            weigh_state(i - 3, helper)
-            add_products(i - 3, helper)
             if last_blend:
-                make_num_and_den(GROUPS - 1)
-                multiply_num_den(GROUPS - 1)
+                weigh_state(i - 3, helper)
+                scale_v(i - 3)
+                add_f2(i - 3)
+                add_f2_v(i - 3, helper)
+                multiply_num_den(i - 3, nc.vector)
+            else:
+                scale_v(i - 3)
+                weigh_state(i - 3, helper)
+                add_f2_v(i - 3, helper)
+            if i - 4 < LN_BATCH:
+                multiply_num_den(i - 4, nc.gpsimd)
             if (i - 1, 0) not in VECTOR_HALVES:
-                group_words(i - 1, 0, nc.scalar.copy)
+                group_words(i - 1, 0, nc.scalar.copy, VECTOR_ROWS if i - 1 in range(FIRST_SHARED, LAST_SHARED) else 0)
             exponentials(i - 2)
             if (i - 1, 1) not in VECTOR_HALVES:
                 group_words(i - 1, 1, nc.scalar.copy)
             if i == 1:
                 nc.scalar.activation(out=column_ratio[:], in_=column_ratio[:], func=ACT.Exp, scale=-1.0)
-            for g in states_of_step(i):
-                prepare_state(g)
             mix_x(i)
             if i == 0:
                 spread_state_rows()
                 quantise_weights()
+            for g in states_of_step(i):
+                prepare_state(g)
             transpose("x", i + 1, 0)
             transpose("x", i + 1, 1)
             last_step = i == GROUPS + 3
             for g in inverted[: None if last_step else 1 if i < GROUPS else 2]:
                 inverses([g])
-                divide(g, nc.vector if last_step and g % 2 else nc.gpsimd)
+                divide(g, nc.vector if last_step else nc.gpsimd)
                 inverted.remove(g)
             quantise(i - 1)
             project(i - 1)

from contextlib import ExitStack

import concourse.mybir as mybir
from concourse.masks import make_identity

F32 = mybir.dt.float32
BF16 = mybir.dt.bfloat16
U32 = mybir.dt.uint32
U8 = mybir.dt.uint8
FP8X4 = mybir.dt.float8_e4m3fn_x4
ALU = mybir.AluOpType
ACT = mybir.ActivationFunctionType

P = 128
B, D, A = 6144, 512, 128
PACK = 4
HALVES = 2
PAIR = 2
ROWS_PER_PARTITION = B // P
TILES = 4
GROUP = TILES * P
GROUPS = B // GROUP
STATES_PER_STEP = 4
FIRST_PIECES = 2
LN_BATCH = 5
VECTOR_ROWS = 176
FIRST_SHARED, LAST_SHARED = 1, 12
VECTOR_HALVES = ((0, 1), (LN_BATCH + 3, 0))

FLOPS = 2 * 2 * B * D * A


def tile_rwkv_attention_pa_t_kernel(
    tc,
    x,
    saved_x,
    saved_a,
    saved_b,
    saved_p,
    time_decay,
    time_first,
    k_mixed,
    v_mixed,
    key_weight,
    value_weight,
    wkv_out,
    aa_out,
    bb_out,
    p2_out,
):
    nc = tc.nc

    def by_partition(dram):
        return dram.rearrange("(p n) c -> p n c", n=ROWS_PER_PARTITION)

    x_rows, sx_rows = by_partition(x), by_partition(saved_x)
    sa_rows, sb_rows, sp_rows = by_partition(saved_a), by_partition(saved_b), by_partition(saved_p)
    wkv_rows, aa_rows = by_partition(wkv_out), by_partition(aa_out)
    bb_rows, p2_rows = by_partition(bb_out), by_partition(p2_out)

    def rows_of(g):
        return slice(g * TILES, (g + 1) * TILES)

    def in_range(g):
        return 0 <= g < GROUPS

    with ExitStack() as stack:
        const = stack.enter_context(tc.tile_pool(name="const", bufs=1))
        sbuf = stack.enter_context(tc.tile_pool(name="sbuf", bufs=2))
        psum = stack.enter_context(tc.psum_pool(name="psum", bufs=1))
        stack.enter_context(tc.manual_schedule())

        one = const.tile([P, 1], F32, name="one")
        nc.vector.memset(one[:], 1.0)
        table_loader = const.tile([P, 1], F32, name="table_loader")
        nc.scalar.activation(out=table_loader[:], in_=one[:], func=ACT.Exp)

        mix_bf16 = const.tile([P, 2, 16], BF16, name="mix_bf16")
        for c, vector in enumerate((k_mixed, v_mixed)):
            nc.sync.dma_start(out=mix_bf16[:, c, 0:PACK], in_=vector.rearrange("(q t) -> q t", t=PACK))
        mix = const.tile([P, 2, PACK], F32, name="mix")
        nc.vector.tensor_copy(out=mix[:], in_=mix_bf16[:, :, 0:PACK])
        one_minus_mix = const.tile([P, 2, PACK], F32, name="one_minus_mix")
        nc.vector.tensor_scalar(
            out=one_minus_mix[:], in0=mix[:], scalar1=-1.0, scalar2=1.0, op0=ALU.mult, op1=ALU.add
        )

        identity = const.tile([P, P], F32, name="identity")
        make_identity(nc, identity[:])

        state_rows = const.tile([P, 2, A], BF16, name="state_rows")
        nc.gpsimd.memset(state_rows[:], 0.0)
        ones = const.tile([P, P], BF16, name="ones")
        nc.gpsimd.memset(ones[:], 1.0)

        w_raw = const.tile([P, 2, PACK, A], BF16, name="w_raw")
        w_grouped = const.tile([P, 2, A, PACK], BF16, name="w_grouped", align_bytes=64)
        w_codes = const.tile([P, 2 * A], U32, name="w_codes", align_bytes=64)
        w_scales = const.tile([P, 2 * A], U8, name="w_scales", align_bytes=64)
        decay_bc = const.tile([P, A], F32, name="decay_bc")
        column_ratio = const.tile([P, A], F32, name="column_ratio")

        def load_constants():
            nc.sync.dma_start(out=state_rows[0:1, 0, :], in_=time_decay.unsqueeze(0))
            nc.sync.dma_start(out=state_rows[0:1, 1, :], in_=time_first.unsqueeze(0))
            for c, weight in enumerate((key_weight, value_weight)):
                nc.sync.dma_start(out=w_raw[:, c], in_=weight.rearrange("(q t) a -> q t a", t=PACK))

        def spread_state_rows():
            spread = psum.tile([P, 2, A], F32, name="spread", tag="k")
            nc.tensor.matmul(
                out=spread[:].rearrange("p v a -> p (v a)"),
                lhsT=ones[:],
                rhs=state_rows[:].rearrange("p v a -> p (v a)"),
                start=True,
                stop=True,
            )
            nc.vector.tensor_copy(out=decay_bc[:], in_=spread[:, 0, :])
            nc.vector.tensor_tensor(out=column_ratio[:], in0=spread[:, 1, :], in1=decay_bc[:], op=ALU.add)

        def quantise_weights():
            for c in range(2):
                nc.vector.tensor_copy(out=w_grouped[:, c], in_=w_raw[:, c].rearrange("q t a -> q a t"))
            nc.vector.quantize_mx(
                out=w_codes[:].bitcast(FP8X4),
                scales=w_scales[:],
                in_=w_grouped[:].rearrange("q c a t -> q (c a t)"),
            )

        def over_tiles(row):
            return row[:].unsqueeze(1).to_broadcast([P, TILES, A])

        sp_all = const.tile([P, ROWS_PER_PARTITION, A], BF16, name="sp_all")

        live = {}

        def new(name, g, shape, dtype, bufs, pool=sbuf, align_bytes=None):
            live[name, g] = pool.tile(
                shape, dtype, name="%s_%d" % (name, g), tag=name, bufs=bufs, align_bytes=align_bytes
            )
            return live[name, g]

        def new_f32(name, g, bufs):
            return new(name, g, [P, TILES, A], F32, bufs)

        def load(g):
            if not in_range(g):
                return
            pieces = FIRST_PIECES if g == 0 else 1
            for name, dram in (("sx", sx_rows), ("x", x_rows)):
                rows = new(name, g, [P, TILES, D], BF16, 3)
                for piece in range(pieces):
                    part = slice(piece * TILES // pieces, (piece + 1) * TILES // pieces)
                    nc.sync.dma_start(out=rows[:, part, :], in_=dram[:, rows_of(g), :][:, part, :])
            sab = new("sab", g, [P, 2, TILES * A], BF16, 6)
            for which, rows in enumerate((sa_rows, sb_rows)):
                nc.sync.dma_start(
                    out=sab[:, which].rearrange("p (j a) -> p j a", a=A), in_=rows[:, rows_of(g), :]
                )

        def states_of_step(i):
            return range(STATES_PER_STEP * i, min(STATES_PER_STEP * (i + 1), GROUPS)) if i >= 0 else ()

        def load_states(i):
            for g in states_of_step(i):
                nc.sync.dma_start(out=sp_all[:, rows_of(g), :], in_=sp_rows[:, rows_of(g), :])

        def transpose(name, g, u):
            if not in_range(g):
                return
            words = live[name, g][:].bitcast(F32)
            bank = new("%s_t%d" % (name, u), g, [P, GROUP], F32, 1, pool=psum)
            for j in range(TILES):
                nc.tensor.transpose(
                    out=bank[:, j * P : (j + 1) * P],
                    in_=words[:, j, u::HALVES],
                    identity=identity[:],
                )

        def value_of_word(bank, e):
            return bank[:].bitcast(BF16).rearrange("q (r e) -> q e r", e=PAIR)[:, e, :]

        def scale_saved_x(g, u):
            if not in_range(g):
                return
            for c in range(2):
                new("scaled%d%d" % (c, u), g, [P, PAIR, GROUP], F32, 2)
            for e in range(PAIR):
                for c in range(2):
                    t = PAIR * u + e
                    nc.scalar.activation(
                        out=live["scaled%d%d" % (c, u), g][:, e, :],
                        in_=value_of_word(live["sx_t%d" % u, g], e),
                        func=ACT.Copy,
                        scale=one_minus_mix[:, c, t : t + 1],
                    )

        def mix_x(g):
            if not in_range(g):
                return
            for c in range(2):
                new("mixed%d" % c, g, [P, PACK, GROUP], BF16, 2)
            for t in range(PACK):
                u, e = divmod(t, PAIR)
                for c in range(2):
                    nc.vector.scalar_tensor_tensor(
                        out=live["mixed%d" % c, g][:, t, :],
                        in0=value_of_word(live["x_t%d" % u, g], e),
                        scalar=mix[:, c, t : t + 1],
                        in1=live["scaled%d%d" % (c, u), g][:, e, :],
                        op0=ALU.mult,
                        op1=ALU.add,
                    )

        def group_words(g, c, engine_copy, first_row=0, last_row=GROUP):
            if not in_range(g):
                return
            if ("grouped%d" % c, g) not in live:
                new("grouped%d" % c, g, [P, GROUP, PACK], BF16, 1, align_bytes=64)
            rows = slice(first_row, last_row)
            engine_copy(
                out=live["grouped%d" % c, g][:, rows, :].rearrange("q (n i) t -> q n t i", i=4),
                in_=live["mixed%d" % c, g][:, :, rows].rearrange("q t (n i) -> q n t i", i=4),
            )

        def quantise(g):
            if not in_range(g):
                return
            for c in range(2):
                codes = new("codes%d" % c, g, [P, GROUP], U32, 2, align_bytes=64)
                scales = new("scales%d" % c, g, [P, GROUP], U8, 2, align_bytes=64)
                nc.vector.quantize_mx(
                    out=codes[:].bitcast(FP8X4),
                    scales=scales[:],
                    in_=live["grouped%d" % c, g][:].rearrange("q r t -> q (r t)"),
                )

        def project(g):
            if not in_range(g):
                return
            for c, (name, bufs) in enumerate((("k", 1), ("v", 2))):
                bank = new(name, g, [P, TILES, A], F32, bufs, pool=psum)
                for j in range(TILES):
                    tile_rows = slice(j * P, (j + 1) * P)
                    nc.tensor.matmul_mx(
                        out=bank[:, j, :],
                        lhsT=live["codes%d" % c, g][:, tile_rows].bitcast(FP8X4),
                        lhsT_scale=live["scales%d" % c, g][:, tile_rows],
                        rhs=w_codes[:, c * A : (c + 1) * A].bitcast(FP8X4),
                        rhs_scale=w_scales[:, c * A : (c + 1) * A],
                        start=True,
                        stop=True,
                    )

        def prepare_state(g):
            if not in_range(g):
                return
            nc.gpsimd.tensor_tensor(
                out=new_f32("w2", g, 12)[:], in0=sp_all[:, rows_of(g), :], in1=over_tiles(decay_bc), op=ALU.add
            )

        def compare(g):
            if not in_range(g):
                return
            k, w2 = live["k", g], live["w2", g]
            nc.vector.tensor_tensor(out=new_f32("d2", g, 2)[:], in0=k[:], in1=w2[:], op=ALU.subtract)
            nc.vector.tensor_tensor(out=new_f32("p2", g, 2)[:], in0=k[:], in1=w2[:], op=ALU.max)
            nc.sync.dma_start(out=p2_rows[:, rows_of(g), :], in_=live["p2", g][:])

        def exponentials(g):
            if not in_range(g):
                return
            d2 = live["d2", g]
            nc.scalar.activation(out=new_f32("exp_up", g, 3)[:], in_=d2[:], func=ACT.Exp)
            nc.scalar.activation(out=new_f32("exp_down", g, 2)[:], in_=d2[:], func=ACT.Exp, scale=-1.0)

        def both(tile):
            return tile[:].rearrange("p j a -> p (j a)").unsqueeze(1).to_broadcast([P, 2, TILES * A])

        def half(pair, which):
            return pair[:, which].rearrange("p (j a) -> p j a", a=A)

        stt = nc.vector.scalar_tensor_tensor

        def scale_state(g):
            if not in_range(g):
                return
            state = new("state", g, [P, 4, TILES * A], F32, 3)
            stt(
                out=state[:, 0:2], in0=both(live["exp_down", g]), scalar=1.0, in1=live["sab", g][:], op0=ALU.min, op1=ALU.mult
            )

        def weigh_state(g, engine):
            if not in_range(g):
                return

            def by_tile(parts):
                return live["state", g][:, parts].rearrange("p w (j a) -> p (w j) a", a=A)

            engine.tensor_tensor(
                out=by_tile(slice(2, 4)),
                in0=by_tile(slice(0, 2)),
                in1=column_ratio[:].unsqueeze(1).to_broadcast([P, 2 * TILES, A]),
                op=ALU.mult,
            )

        def scale_v(g):
            if not in_range(g):
                return
            f2_v = new_f32("f2_v", g, 2)
            stt(out=f2_v[:], in0=live["exp_up", g][:], scalar=1.0, in1=live["v", g][:], op0=ALU.min, op1=ALU.mult)

        def add_f2_v(g, engine):
            if not in_range(g):
                return
            aa_num = new("aa_num", g, [P, 2, TILES * A], F32, 2)
            engine.tensor_tensor(out=aa_num[:], in0=live["state", g][:, 0::2], in1=both(live["f2_v", g]), op=ALU.add)
            nc.sync.dma_start(out=aa_rows[:, rows_of(g), :], in_=half(aa_num, 0))

        def add_f2(g):
            if not in_range(g) or ("bb_den", g) in live:
                return
            bb_den = new("bb_den", g, [P, 2, TILES * A], F32, 2)
            stt(
                out=bb_den[:], in0=both(live["exp_up", g]), scalar=1.0, in1=live["state", g][:, 1::2], op0=ALU.min, op1=ALU.add
            )
            nc.sync.dma_start(out=bb_rows[:, rows_of(g), :], in_=half(bb_den, 0))

        def multiply_num_den(g, engine):
            if not in_range(g) or ("num_den", g) in live:
                return
            engine.tensor_tensor(
                out=new_f32("num_den", g, 7)[:],
                in0=half(live["aa_num", g], 1),
                in1=half(live["bb_den", g], 1),
                op=ALU.mult,
            )

        def square_den(g):
            if not in_range(g) or ("inv_den2", g) in live:
                return
            nc.scalar.activation(out=new_f32("inv_den2", g, 7)[:], in_=half(live["bb_den", g], 1), func=ACT.Square)

        def logarithms(groups):
            for g in groups:
                nc.scalar.activation(out=live["inv_den2", g][:], in_=live["inv_den2", g][:], func=ACT.Ln)

        def inverses(groups):
            for g in groups:
                nc.scalar.activation(out=live["inv_den2", g][:], in_=live["inv_den2", g][:], func=ACT.Exp, scale=-1.0)

        def divide(g, engine):
            product = live["num_den", g]
            engine.tensor_tensor(out=product[:], in0=product[:], in1=live["inv_den2", g][:], op=ALU.mult)
            nc.sync.dma_start(out=wkv_rows[:, rows_of(g), :], in_=product[:])

        inverted = []
        for i in range(-2, GROUPS + 4):
            load(i + 2)
            load_states(i + 2)
            if i == -2:
                load_constants()
            scale_saved_x(i, 0)
            scale_saved_x(i, 1)
            transpose("sx", i + 1, 0)
            transpose("sx", i + 1, 1)
            tail = i >= GROUPS
            if tail:
                compare(i - 2)
            last_blend = i - 3 == GROUPS - 1
            add_f2(i - 4)
            for c in range(2):
                if (i - 1, c) in VECTOR_HALVES:
                    group_words(i - 1, c, nc.vector.tensor_copy)
                elif c == 0 and i - 1 in range(FIRST_SHARED, LAST_SHARED):
                    group_words(i - 1, c, nc.vector.tensor_copy, 0, VECTOR_ROWS)
            scale_state(i - 3)
            if i - 4 >= LN_BATCH:
                multiply_num_den(i - 4, nc.vector)
            helper = nc.gpsimd if i - 3 < GROUPS - 2 else nc.vector
            if not tail:
                compare(i - 2)
            if last_blend:
                weigh_state(i - 3, helper)
                scale_v(i - 3)
                add_f2(i - 3)
                add_f2_v(i - 3, helper)
                multiply_num_den(i - 3, nc.vector)
            else:
                scale_v(i - 3)
                weigh_state(i - 3, helper)
                add_f2_v(i - 3, helper)
            if i - 4 < LN_BATCH:
                multiply_num_den(i - 4, nc.gpsimd)
            if (i - 1, 0) not in VECTOR_HALVES:
                group_words(i - 1, 0, nc.scalar.copy, VECTOR_ROWS if i - 1 in range(FIRST_SHARED, LAST_SHARED) else 0)
            exponentials(i - 2)
            if (i - 1, 1) not in VECTOR_HALVES:
                group_words(i - 1, 1, nc.scalar.copy)
            if i == 1:
                nc.scalar.activation(out=column_ratio[:], in_=column_ratio[:], func=ACT.Exp, scale=-1.0)
            mix_x(i)
            if i == 0:
                spread_state_rows()
                quantise_weights()
            for g in states_of_step(i):
                prepare_state(g)
            transpose("x", i + 1, 0)
            transpose("x", i + 1, 1)
            last_step = i == GROUPS + 3
            for g in inverted[: None if last_step else 1 if i < GROUPS else 2]:
                inverses([g])
                divide(g, nc.vector if last_step else nc.gpsimd)
                inverted.remove(g)
            quantise(i - 1)
            project(i - 1)
            square_den(i - 4)
            if last_blend:
                logarithms([GROUPS - 3, GROUPS - 2])
                square_den(GROUPS - 1)
                logarithms([GROUPS - 1])
                inverted.extend([GROUPS - 3, GROUPS - 2, GROUPS - 1])
            for first, end in ((0, LN_BATCH), (LN_BATCH, GROUPS - 3)):
                if i - 4 == end - 1:
                    logarithms(range(first, end))
                    inverted.extend(range(first, end))
